import numpy as np
import ml_dtypes


def mxq(x, axis, fmt="e4m3"):
    dtype, down = {"e4m3": (ml_dtypes.float8_e4m3fn, 7), "e5m2": (ml_dtypes.float8_e5m2, 14)}[fmt]
    v = np.moveaxis(np.asarray(x, np.float32).astype(ml_dtypes.bfloat16).astype(np.float64), axis, -1)
    blocks = v.reshape(v.shape[:-1] + (-1, 32))
    amax = np.abs(blocks).max(-1, keepdims=True)
    byte = np.maximum(np.where(amax > 0, np.frexp(amax)[1] - 1 + 127, 0) - down, 1)
    scale = np.exp2(byte - 127.0)
    codes = (blocks / scale).astype(np.float32).astype(dtype).astype(np.float64)
    return np.moveaxis((codes * scale).reshape(v.shape), -1, axis)


WIDE = False


def mx_kscale(k):
    if not WIDE:
        return np.ones(k)
    levels = np.array([10, -10, 5, -5, 0])
    a = np.random.permutation(np.resize(levels, k // 512 * 4)).reshape(k // 512, 4)
    idx = np.arange(k)
    return np.exp2(a[idx // 512, idx % 128 // 32])


BF16 = ml_dtypes.bfloat16


def bf(x):
    return np.asarray(x, np.float32).astype(BF16)


def f64(x):
    return np.asarray(x).astype(np.float64)


E2M1 = np.array([0.0, 0.5, 1.0, 1.5, 2.0, 3.0, 4.0, 6.0, -0.0, -0.5, -1.0, -1.5, -2.0, -3.0, -4.0, -6.0])


def pack_weight(w, fmt):
    k, n = w.shape
    w = f64(bf(w)).reshape(k // 32, 32, n)
    amax = np.abs(w).max(1)
    if fmt == "e4m3":
        byte = np.frexp(amax)[1] - 1 + 127 - 7
    else:
        mant, ex = np.frexp(amax / 6.0)
        byte = np.where(mant > 0.5, ex, ex - 1) + 127
    byte = np.clip(np.where(amax > 0, byte, 1), 1, 254)
    scaled = (w * np.exp2(127.0 - byte)[:, None, :]).reshape(k, n).astype(np.float32)
    by_word = np.ascontiguousarray(scaled.reshape(k // 512, 128, 4, n).transpose(0, 1, 3, 2))
    if fmt == "e4m3":
        words = by_word.astype(ml_dtypes.float8_e4m3fn).view(np.uint8)
    else:
        c = by_word.astype(ml_dtypes.float4_e2m1fn).view(np.uint8) & 0xF
        words = c[..., 0::2] | (c[..., 1::2] << 4)
    return np.ascontiguousarray(words), np.ascontiguousarray(byte.astype(np.uint8).reshape(k // 512, 16, n))


def unpack_weight(words, scales, fmt):
    g, p, n, _ = words.shape
    if fmt == "e4m3":
        vals = np.ascontiguousarray(words).view(ml_dtypes.float8_e4m3fn).astype(np.float64)
    else:
        nib = np.empty((g, p, n, 4), np.uint8)
        nib[..., 0::2] = words & 0xF
        nib[..., 1::2] = words >> 4
        vals = E2M1[nib]
    vals = vals * np.repeat(np.exp2(scales.astype(np.float64) - 127.0), 8, axis=1)[..., None]
    return vals.transpose(0, 1, 3, 2).reshape(g * 512, n)


B, T, E, Q = 4, 512, 1024, 512
EPS_RMS = 1.1920929e-07


def silu(t):
    return t * (1.0 / (1.0 + np.exp(-t)))


def rms_norm(t):
    return t * (1.0 / np.sqrt(np.mean(t * t, axis=-1, keepdims=True) + EPS_RMS))


def w_norm(w, n):
    target_std = n ** (-0.5)
    return w * (target_std / (np.std(w, ddof=1) + 1e-08))


def setup_inputs():
    s = mx_kscale(E)
    u = s / s.min()
    row = np.where(u > 1.0, np.sqrt(EPS_RMS) / u, np.sqrt(T / (B * E)) * np.exp2(np.random.uniform(-1.0, 1.0, E)))
    ao = bf(np.random.standard_normal((E, E)) * row[:, None])
    w_swiglu = bf((np.random.standard_normal((E, 2 * Q)) / np.sqrt(Q) * u[:, None]).reshape(2 * E, Q))
    w_out = bf(np.random.standard_normal((E, E)) / np.sqrt(E) * u)
    out_w = (np.random.standard_normal((E, E)) * np.sqrt(E) + 2.0) / E * u[:, None]
    out_w_words, out_w_scales = pack_weight(np.ascontiguousarray(out_w.T), "e4m3")
    tao = bf(np.random.uniform(0.5, 1.5, (2, 1)) * np.random.choice([-1.0, 1.0], (2, 1)))
    return {"ao": ao,
            "w_swiglu": w_swiglu,
            "w_out": w_out,
            "out_w_words": out_w_words,
            "out_w_scales": out_w_scales,
            "tao": tao}


def reference(ao, w_swiglu, w_out, out_w_words, out_w_scales, tao):
    ws, wo = f64(w_swiglu), f64(w_out)
    g = np.clip(np.abs(f64(tao)), 1e-08, 1.0)
    beta, gamma = g[0], g[1]
    aoq = mxq(rms_norm(f64(ao)), 0, "e4m3")
    owq = unpack_weight(out_w_words, out_w_scales, "e4m3")
    n2 = silu(mxq(ws.reshape(E, 2 * Q).T, 1, "e4m3") @ aoq)
    n2 = mxq(n2, 1, "e4m3") @ owq
    ws_new = w_norm(ws + n2.T.reshape(2 * E, Q), Q) * beta
    n3 = silu(mxq(wo, 1, "e4m3") @ aoq)
    wo_new = w_norm(wo + (mxq(n3, 1, "e4m3") @ owq), Q) * gamma
    return ws_new, wo_new

@@ -1,0 +1,344 @@
+from contextlib import ExitStack
+
+import concourse.mybir as mybir
+from concourse.masks import make_identity
+
+FP8X4 = mybir.dt.float8_e4m3fn_x4
+BF16 = mybir.dt.bfloat16
+F32 = mybir.dt.float32
+I32 = mybir.dt.int32
+U32 = mybir.dt.uint32
+U8 = mybir.dt.uint8
+ACT = mybir.ActivationFunctionType
+ALU = mybir.AluOpType
+AXIS = mybir.AxisListType
+
+P = 128
+E = 1024
+PACK = 4
+K_PASS = P * PACK
+PASSES = E // K_PASS
+BLOCK = 512
+BLOCKS = 2 * E // BLOCK
+BANKS = BLOCK // P * PASSES
+ROW_TILES = E // P
+EPS_RMS = 1.1920929e-07
+EPS_STD = 1e-08
+COUNT = E * E
+TARGET_STD = 512.0 ** -0.5
+LAG = 2
+STATS_LAG = 3
+
+FLOPS = 4 * 2 * E * E * E
+
+
+def tile_retentionmechanism_pc_kernel(
+    tc, ao, w_swiglu, w_out, out_w_words, out_w_scales, tao, out_0, out_1
+):
+    nc = tc.nc
+    with ExitStack() as ctx:
+        ctx.enter_context(tc.manual_schedule())
+        consts = ctx.enter_context(tc.tile_pool(name="consts", bufs=1))
+        keep = ctx.enter_context(tc.tile_pool(name="keep", bufs=1))
+        stage = ctx.enter_context(tc.tile_pool(name="stage", bufs=2))
+        psum = ctx.enter_context(tc.psum_pool(name="psum", bufs=4))
+
+        v_dram = w_swiglu.rearrange("(d h) q -> d (h q)", h=2)
+        out1_dram = out_0.rearrange("(d h) q -> d (h q)", h=2)
+
+        def by_word_order(x):
+            return x.rearrange("(g u p h) c -> g u p h c", g=PASSES, u=2, p=P, h=2)
+
+        def by_row_tile(x):
+            return x.rearrange("(r p) c -> p r c", p=P)
+
+        eps_rms = consts.tile([P, 1], F32)
+        nc.gpsimd.memset(eps_rms[:], EPS_RMS)
+        ident = consts.tile([P, P], F32)
+        make_identity(nc, ident[:])
+        ones = consts.tile([P, P], F32)
+        nc.gpsimd.memset(ones[:], 1.0)
+        half = consts.tile([P, 1], F32)
+        nc.gpsimd.memset(half[:], 0.5)
+        warm = consts.tile([P, 2], F32)
+        nc.scalar.activation(out=warm[:, 0:1], in_=eps_rms[:], func=ACT.Sqrt)
+
+        head = keep.tile([P, 2 * PASSES * PACK * E], BF16, tag="big", align_bytes=64)
+        ao_sb = head[:, 0 : PASSES * PACK * E].rearrange(
+            "p (g u h c) -> p g u h c", g=PASSES, u=2, h=2
+        )
+        a_grouped = head[:, PASSES * PACK * E :].rearrange(
+            "p (g2 g x) -> p g2 g x", g2=PASSES, g=PASSES
+        )
+        ao_rows = by_word_order(ao)
+        for g in range(PASSES):
+            for u in range(2):
+                nc.sync.dma_start(out=ao_sb[:, g, u], in_=ao_rows[g, u])
+
+        tao_sb = consts.tile([P, 2], BF16)
+        nc.scalar.dma_start(out=tao_sb[:], in_=tao.rearrange("a b -> (a b)").partition_broadcast(P))
+
+        wo_sb = keep.tile([P, ROW_TILES, E], BF16)
+        wo_rows = by_row_tile(w_out)
+        for r in range(0, ROW_TILES, 2):
+            nc.sync.dma_start(out=wo_sb[:, r : r + 2, :], in_=wo_rows[:, r : r + 2, :])
+
+        w_codes = keep.tile([P, PASSES, E], U32, align_bytes=64)
+        w_scales = keep.tile([P, PASSES, E], U8, align_bytes=64)
+        nc.vector.memset(w_scales[:].rearrange("p g n -> p (g n)").bitcast(I32), 0)
+        for quad in range(4):
+            nc.sync.dma_start(
+                out=w_scales[32 * quad : 32 * quad + 4].bitcast(I32),
+                in_=out_w_scales[:, 4 * quad : 4 * quad + 4, :].rearrange("g r n -> r g n").bitcast(I32),
+            )
+        for g2 in range(PASSES):
+            nc.sync.dma_start(
+                out=w_codes[:, g2, :].bitcast(I32),
+                in_=out_w_words[g2].rearrange("p n t -> p (n t)").bitcast(I32),
+            )
+
+        vq_sb = keep.tile([P, PASSES, 2, 2, E], BF16)
+        v_rows = by_word_order(v_dram)
+        for g in range(PASSES):
+            for u in range(2):
+                nc.sync.dma_start(out=vq_sb[:, g, u], in_=v_rows[g, u])
+        v_sb = keep.tile([P, ROW_TILES, E], BF16)
+        v_tiles = by_row_tile(v_dram)
+        for r in range(0, ROW_TILES, 2):
+            nc.sync.dma_start(out=v_sb[:, r : r + 2, :], in_=v_tiles[:, r : r + 2, :])
+
+        sumsq = consts.tile([P, 2, 8], F32)
+        rms = consts.tile([P, 2, 8], F32)
+        rstd = consts.tile([P, 2, 8], F32)
+        for g in range(PASSES):
+            for u in range(2):
+                col = 2 * g + u
+                sq_s = stage.tile([P, E], BF16, tag="sq_s", bufs=3)
+                nc.scalar.activation(
+                    out=sq_s[:], in_=ao_sb[:, g, u, 0, :], func=ACT.Square,
+                    accum_out=sumsq[:, 0, col : col + 1],
+                )
+                sq_v = stage.tile([P, E], BF16, tag="sq_v")
+                nc.vector.scalar_tensor_tensor(
+                    out=sq_v[:], in0=ao_sb[:, g, u, 1, :], scalar=1.0, in1=ao_sb[:, g, u, 1, :],
+                    op0=ALU.mult, op1=ALU.mult, accum_out=sumsq[:, 1, col : col + 1],
+                )
+            nc.scalar.activation(
+                out=rms[:, :, 2 * g : 2 * g + 2], in_=sumsq[:, :, 2 * g : 2 * g + 2], func=ACT.Sqrt,
+                scale=1.0 / E, bias=eps_rms[:],
+            )
+        nc.scalar.activation(out=warm[:, 1:2], in_=eps_rms[:], func=ACT.Silu)
+
+        for g in range(PASSES):
+            nc.vector.reciprocal(out=rstd[:, :, 2 * g : 2 * g + 2], in_=rms[:, :, 2 * g : 2 * g + 2])
+            for u in range(2):
+                for h in range(2):
+                    nc.vector.tensor_scalar(
+                        out=ao_sb[:, g, u, h, :], in0=ao_sb[:, g, u, h, :],
+                        scalar1=rstd[:, h, 2 * g + u : 2 * g + u + 1], scalar2=None, op0=ALU.mult,
+                    )
+
+        x_codes = keep.tile([P, BLOCKS, PASSES, BLOCK], U32, align_bytes=64)
+        x_scales = keep.tile([P, BLOCKS, PASSES, BLOCK], U8, align_bytes=64)
+
+        def quantise_block(blk, grouped):
+            nc.vector.quantize_mx(
+                out=x_codes[:, blk].rearrange("p g c -> p (g c)").bitcast(FP8X4),
+                scales=x_scales[:, blk].rearrange("p g c -> p (g c)"),
+                in_=grouped[:].rearrange("p g x -> p (g x)"),
+            )
+
+        def transpose_w_out_block(blk):
+            grouped = stage.tile([P, PASSES, PACK * BLOCK], BF16, tag="x_grouped", align_bytes=64)
+            grouped_words = grouped[:].bitcast(F32).rearrange("p g (i u) -> p g i u", u=2)
+            for l in range(BLOCK // P):
+                words = wo_sb[:, blk * (BLOCK // P) + l, :].bitcast(F32)
+                flipped = psum.tile([P, PACK, P], F32, tag="first")
+                for b in range(PACK):
+                    nc.tensor.transpose(flipped[:, b, :], words[:, b * P : (b + 1) * P], ident[:])
+                nc.scalar.copy(
+                    out=grouped_words[:, :, l * P : (l + 1) * P, :],
+                    in_=flipped[:].rearrange("p (g u) i -> p g i u", u=2),
+                )
+            return grouped
+
+        wo_grouped = [transpose_w_out_block(blk) for blk in range(2)]
+
+        a_codes = keep.tile([P, PASSES, PASSES, K_PASS], U32, align_bytes=64)
+        a_scales = keep.tile([P, PASSES, PASSES, K_PASS], U8, align_bytes=64)
+
+        def regroup_a(g2, g):
+            rows = ao_sb[:, g].rearrange("p u h c -> p (u h) c")[:, :, g2 * K_PASS : (g2 + 1) * K_PASS]
+            nc.vector.tensor_copy(
+                out=a_grouped[:, g2, g, :].rearrange("p (s c t) -> p s c t", s=PACK, t=PACK),
+                in_=rows.rearrange("p t (c s) -> p s c t", s=PACK),
+            )
+
+        def quantise_a(g2, g):
+            nc.vector.quantize_mx(
+                out=a_codes[:, g2, g, :].bitcast(FP8X4), scales=a_scales[:, g2, g, :],
+                in_=a_grouped[:, g2, g, :],
+            )
+
+        for g2 in range(PASSES):
+            for g in range(PASSES):
+                regroup_a(g2, g)
+            quantise_block(g2, wo_grouped[g2])
+            for g in range(PASSES):
+                quantise_a(g2, g)
+
+        gate = consts.tile([P, 2], F32)
+        nc.vector.tensor_scalar(out=gate[:], in0=tao_sb[:], scalar1=-1.0, scalar2=None, op0=ALU.mult)
+        nc.vector.tensor_tensor(out=gate[:], in0=gate[:], in1=tao_sb[:], op=ALU.max)
+        nc.vector.tensor_scalar(out=gate[:], in0=gate[:], scalar1=1e-08, scalar2=1.0, op0=ALU.max, op1=ALU.min)
+
+        def regroup_v_block(blk):
+            cols = slice((blk - 2) * BLOCK, (blk - 1) * BLOCK)
+            grouped = stage.tile([P, PASSES, PACK * BLOCK], BF16, tag="x_grouped", align_bytes=64)
+            for g in range(PASSES):
+                rows = vq_sb[:, g].rearrange("p u h c -> p (u h) c")[:, :, cols]
+                nc.vector.tensor_copy(
+                    out=grouped[:, g, :].rearrange("p (c i t) -> p c t i", i=4, t=PACK),
+                    in_=rows.rearrange("p t (c i) -> p c t i", i=4),
+                )
+            quantise_block(blk, grouped)
+
+        z2 = keep.tile([P, ROW_TILES, E], F32)
+        z_of = {1: z2}
+        weight_of = {0: v_sb, 1: wo_sb}
+        z_sum = {}
+        z_sumsq = {}
+        for o in range(2):
+            z_sum[o] = consts.tile([P, 2 * BANKS], F32, name="z_sum%d" % o)
+            z_sumsq[o] = consts.tile([P, BANKS], F32, name="z_sumsq%d" % o)
+        n_grouped = {}
+        n_codes = {}
+        n_scales = {}
+
+        def first_product_bank(k):
+            blk, g2, cb = k // BANKS, (k % BANKS) // (BLOCK // P), k % (BLOCK // P)
+            if k % BANKS == 0:
+                n_grouped[blk] = stage.tile([P, PASSES, BLOCK, PACK], BF16, tag="n_grouped", name="n_grouped", align_bytes=64)
+                n_codes[blk] = stage.tile([P, PASSES, BLOCK], U32, tag="n_codes", name="n_codes", bufs=3, align_bytes=64)
+                n_scales[blk] = stage.tile([P, PASSES, BLOCK], U8, tag="n_scales", name="n_scales", bufs=3, align_bytes=64)
+            cols = slice(cb * P, (cb + 1) * P)
+            bank = psum.tile([P, PACK, P], F32, tag="first")
+            for s in range(PACK):
+                for g in range(PASSES):
+                    nc.tensor.matmul_mx(
+                        out=bank[:, s, :],
+                        lhsT=a_codes[:, g2, g, s * P : (s + 1) * P].bitcast(FP8X4),
+                        lhsT_scale=a_scales[:, g2, g, s * P : (s + 1) * P],
+                        rhs=x_codes[:, blk, g, cols].bitcast(FP8X4),
+                        rhs_scale=x_scales[:, blk, g, cols],
+                        start=(g == 0),
+                        stop=(g == PASSES - 1),
+                    )
+            nc.scalar.activation(
+                out=n_grouped[blk][:, g2, cols, :], in_=bank[:].rearrange("p s c -> p c s"), func=ACT.Silu
+            )
+            if cb == BLOCK // P - 1:
+                nc.vector.quantize_mx(
+                    out=n_codes[blk][:, g2, :].bitcast(FP8X4), scales=n_scales[blk][:, g2, :],
+                    in_=n_grouped[blk][:, g2].rearrange("p c s -> p (c s)"),
+                )
+
+        def second_product_bank(k):
+            blk, b = k // BANKS, k % BANKS
+            o = 1 if blk < 2 else 0
+            bank = psum.tile([P, BLOCK], F32, tag="second")
+            if o == 1:
+                r, cols = blk * (BLOCK // P) + b // 2, slice((b % 2) * BLOCK, (b % 2 + 1) * BLOCK)
+                inner = slice((b // 2) * P, (b // 2 + 1) * P)
+                for g2 in range(PASSES):
+                    nc.tensor.matmul_mx(
+                        out=bank[:],
+                        lhsT=n_codes[blk][:, g2, inner].bitcast(FP8X4), lhsT_scale=n_scales[blk][:, g2, inner],
+                        rhs=w_codes[:, g2, cols].bitcast(FP8X4), rhs_scale=w_scales[:, g2, cols],
+                        start=(g2 == 0), stop=(g2 == PASSES - 1),
+                    )
+            else:
+                r, cols = b, slice((blk - 2) * BLOCK, (blk - 1) * BLOCK)
+                inner = slice(b * P, (b + 1) * P)
+                for g2 in range(PASSES):
+                    nc.tensor.matmul_mx(
+                        out=bank[:],
+                        lhsT=w_codes[:, g2, inner].bitcast(FP8X4), lhsT_scale=w_scales[:, g2, inner],
+                        rhs=n_codes[blk][:, g2, :].bitcast(FP8X4), rhs_scale=n_scales[blk][:, g2, :],
+                        start=(g2 == 0), stop=(g2 == PASSES - 1),
+                    )
+            if k == 2 * BANKS:
+                z_of[0] = keep.tile([P, ROW_TILES, E], F32, tag="big", name="z1", align_bytes=64)
+            z = z_of[o]
+            n_th = k % (2 * BANKS)
+            nc.vector.scalar_tensor_tensor(
+                out=z[:, r, cols], in0=bank[:], scalar=1.0, in1=weight_of[o][:, r, cols],
+                op0=ALU.mult, op1=ALU.add, accum_out=z_sum[o][:, n_th : n_th + 1],
+            )
+            if b % 2 == 1:
+                done = z[:, r, :] if o == 1 else z[:, r - 1 : r + 1, cols]
+                sq_s = stage.tile([P, 2 * BLOCK], BF16, tag="sq_s", bufs=3)
+                sq_view = sq_s[:] if o == 1 else sq_s[:].rearrange("p (a c) -> p a c", a=2)
+                nc.scalar.activation(
+                    out=sq_view, in_=done, func=ACT.Square, accum_out=z_sumsq[o][:, n_th // 2 : n_th // 2 + 1]
+                )
+
+        stats = {}
+        totals = {}
+        work_of = {}
+        std_of = {}
+
+        def sum_over_partitions(o):
+            stats[o] = consts.tile([P, 2], F32, name="stats%d" % o)
+            nc.vector.tensor_reduce(out=stats[o][:, 0:1], in_=z_sum[o][:], axis=AXIS.X, op=ALU.add)
+            nc.vector.tensor_reduce(out=stats[o][:, 1:2], in_=z_sumsq[o][:], axis=AXIS.X, op=ALU.add)
+            totals[o] = psum.tile([P, BLOCK], F32, tag="second", name="totals")
+            nc.tensor.matmul(out=totals[o][:, 0:2], lhsT=ones[:], rhs=stats[o][:], start=True, stop=True)
+
+        def variance(o):
+            work = consts.tile([P, 8], F32, name="work%d" % o)
+            work_of[o] = work
+            nc.vector.tensor_copy(out=work[:, 0:2], in_=totals[o][:, 0:2])
+            nc.vector.tensor_scalar(out=work[:, 2:3], in0=work[:, 0:1], scalar1=-1.0 / COUNT, scalar2=None, op0=ALU.mult)
+            nc.vector.scalar_tensor_tensor(
+                out=work[:, 3:4], in0=work[:, 0:1], scalar=work[:, 2:3], in1=work[:, 1:2], op0=ALU.mult, op1=ALU.add
+            )
+            nc.vector.tensor_scalar(
+                out=work[:, 4:5], in0=work[:, 3:4], scalar1=1.0 / (COUNT - 1), scalar2=0.0, op0=ALU.mult, op1=ALU.max
+            )
+            std_of[o] = consts.tile([P, 1], F32, name="std%d" % o)
+            nc.gpsimd.tensor_tensor(out=std_of[o][:], in0=work[:, 4:5], in1=half[:], op=ALU.pow)
+
+        def scale_and_store(o, engine, out_dram):
+            work = work_of[o]
+            nc.vector.tensor_scalar(out=work[:, 5:6], in0=std_of[o][:], scalar1=EPS_STD, scalar2=None, op0=ALU.add)
+            nc.vector.reciprocal(out=work[:, 6:7], in_=work[:, 5:6])
+            nc.vector.tensor_scalar(
+                out=work[:, 7:8], in0=work[:, 6:7], scalar1=gate[:, o : o + 1], scalar2=TARGET_STD, op0=ALU.mult, op1=ALU.mult
+            )
+            rows = by_row_tile(out_dram)
+            for r in range(ROW_TILES):
+                engine.tensor_scalar(
+                    out=z_of[o][:, r, :], in0=z_of[o][:, r, :], scalar1=work[:, 7:8], scalar2=1.0, op0=ALU.mult, op1=ALU.mult
+                )
+                nc.sync.dma_start(out=rows[:, r, :], in_=z_of[o][:, r, :])
+
+        total_banks = BLOCKS * BANKS
+        behind = BANKS + LAG
+        out2_done = 2 * BANKS - 1 + behind + STATS_LAG
+        for step in range(total_banks + behind):
+            if step in (BANKS, 2 * BANKS):
+                regroup_v_block(step // BANKS + 1)
+            if step < total_banks:
+                first_product_bank(step)
+            if step >= behind:
+                second_product_bank(step - behind)
+            if step == out2_done:
+                sum_over_partitions(1)
+            if step == out2_done + 1:
+                variance(1)
+            if step == out2_done + 2:
+                scale_and_store(1, nc.gpsimd, out_1)
+        sum_over_partitions(0)
+        variance(0)
+        scale_and_store(0, nc.vector, out1_dram)

@@ -19,15 +19,16 @@ PACK = 4
 K_PASS = P * PACK
 PASSES = E // K_PASS
 BLOCK = 512
+SLICES = BLOCK // P
 BLOCKS = 2 * E // BLOCK
-BANKS = BLOCK // P * PASSES
+BANKS = SLICES * PASSES
 ROW_TILES = E // P
 EPS_RMS = 1.1920929e-07
 EPS_STD = 1e-08
 COUNT = E * E
 TARGET_STD = 512.0 ** -0.5
 LAG = 2
-STATS_LAG = 3
+SQUARE_LAG = 3
 
 FLOPS = 4 * 2 * E * E * E
 
@@ -52,24 +53,20 @@ def tile_retentionmechanism_pc_kernel(
         def by_row_tile(x):
             return x.rearrange("(r p) c -> p r c", p=P)
 
-        eps_rms = consts.tile([P, 1], F32)
-        nc.gpsimd.memset(eps_rms[:], EPS_RMS)
+        half = consts.tile([P, 1], F32)
+        nc.gpsimd.memset(half[:], 0.5)
+        minus_half = consts.tile([P, 2, 2], F32)
+        nc.gpsimd.memset(minus_half[:], -0.5)
         ident = consts.tile([P, P], F32)
         make_identity(nc, ident[:])
         ones = consts.tile([P, P], F32)
         nc.gpsimd.memset(ones[:], 1.0)
-        half = consts.tile([P, 1], F32)
-        nc.gpsimd.memset(half[:], 0.5)
-        warm = consts.tile([P, 2], F32)
-        nc.scalar.activation(out=warm[:, 0:1], in_=eps_rms[:], func=ACT.Sqrt)
+        warm = consts.tile([P, 1], F32)
+        nc.scalar.activation(out=warm[:], in_=half[:], func=ACT.Silu)
 
         head = keep.tile([P, 2 * PASSES * PACK * E], BF16, tag="big", align_bytes=64)
-        ao_sb = head[:, 0 : PASSES * PACK * E].rearrange(
-            "p (g u h c) -> p g u h c", g=PASSES, u=2, h=2
-        )
-        a_grouped = head[:, PASSES * PACK * E :].rearrange(
-            "p (g2 g x) -> p g2 g x", g2=PASSES, g=PASSES
-        )
+        ao_sb = head[:, 0 : PASSES * PACK * E].rearrange("p (g u h c) -> p g u h c", g=PASSES, u=2, h=2)
+        a_grouped = head[:, PASSES * PACK * E :].rearrange("p (g2 g x) -> p g2 g x", g2=PASSES, g=PASSES)
         ao_rows = by_word_order(ao)
         for g in range(PASSES):
             for u in range(2):
@@ -80,8 +77,12 @@ def tile_retentionmechanism_pc_kernel(
 
         wo_sb = keep.tile([P, ROW_TILES, E], BF16)
         wo_rows = by_row_tile(w_out)
-        for r in range(0, ROW_TILES, 2):
-            nc.sync.dma_start(out=wo_sb[:, r : r + 2, :], in_=wo_rows[:, r : r + 2, :])
+
+        def load_w_out_block(blk):
+            for r in range(blk * SLICES, (blk + 1) * SLICES, 2):
+                nc.sync.dma_start(out=wo_sb[:, r : r + 2, :], in_=wo_rows[:, r : r + 2, :])
+
+        load_w_out_block(0)
 
         w_codes = keep.tile([P, PASSES, E], U32, align_bytes=64)
         w_scales = keep.tile([P, PASSES, E], U8, align_bytes=64)
@@ -96,6 +97,7 @@ def tile_retentionmechanism_pc_kernel(
                 out=w_codes[:, g2, :].bitcast(I32),
                 in_=out_w_words[g2].rearrange("p n t -> p (n t)").bitcast(I32),
             )
+        load_w_out_block(1)
 
         vq_sb = keep.tile([P, PASSES, 2, 2, E], BF16)
         v_rows = by_word_order(v_dram)
@@ -108,7 +110,7 @@ def tile_retentionmechanism_pc_kernel(
             nc.sync.dma_start(out=v_sb[:, r : r + 2, :], in_=v_tiles[:, r : r + 2, :])
 
         sumsq = consts.tile([P, 2, 8], F32)
-        rms = consts.tile([P, 2, 8], F32)
+        mean_sq = consts.tile([P, 2, 8], F32)
         rstd = consts.tile([P, 2, 8], F32)
         for g in range(PASSES):
             for u in range(2):
@@ -123,14 +125,17 @@ def tile_retentionmechanism_pc_kernel(
                     out=sq_v[:], in0=ao_sb[:, g, u, 1, :], scalar=1.0, in1=ao_sb[:, g, u, 1, :],
                     op0=ALU.mult, op1=ALU.mult, accum_out=sumsq[:, 1, col : col + 1],
                 )
-            nc.scalar.activation(
-                out=rms[:, :, 2 * g : 2 * g + 2], in_=sumsq[:, :, 2 * g : 2 * g + 2], func=ACT.Sqrt,
-                scale=1.0 / E, bias=eps_rms[:],
+            pair = slice(2 * g, 2 * g + 2)
+            nc.gpsimd.tensor_scalar(
+                out=mean_sq[:, :, pair], in0=sumsq[:, :, pair],
+                scalar1=1.0 / E, scalar2=EPS_RMS, op0=ALU.mult, op1=ALU.add,
             )
-        nc.scalar.activation(out=warm[:, 1:2], in_=eps_rms[:], func=ACT.Silu)
+            nc.gpsimd.tensor_tensor(out=rstd[:, :, pair], in0=mean_sq[:, :, pair], in1=minus_half[:], op=ALU.pow)
 
-        for g in range(PASSES):
-            nc.vector.reciprocal(out=rstd[:, :, 2 * g : 2 * g + 2], in_=rms[:, :, 2 * g : 2 * g + 2])
+        a_codes = keep.tile([P, PASSES, PASSES, K_PASS], U32, align_bytes=64)
+        a_scales = keep.tile([P, PASSES, PASSES, K_PASS], U8, align_bytes=64)
+
+        def normalise_rows(g):
             for u in range(2):
                 for h in range(2):
                     nc.vector.tensor_scalar(
@@ -138,38 +143,9 @@ def tile_retentionmechanism_pc_kernel(
                         scalar1=rstd[:, h, 2 * g + u : 2 * g + u + 1], scalar2=None, op0=ALU.mult,
                     )
 
-        x_codes = keep.tile([P, BLOCKS, PASSES, BLOCK], U32, align_bytes=64)
-        x_scales = keep.tile([P, BLOCKS, PASSES, BLOCK], U8, align_bytes=64)
-
-        def quantise_block(blk, grouped):
-            nc.vector.quantize_mx(
-                out=x_codes[:, blk].rearrange("p g c -> p (g c)").bitcast(FP8X4),
-                scales=x_scales[:, blk].rearrange("p g c -> p (g c)"),
-                in_=grouped[:].rearrange("p g x -> p (g x)"),
-            )
-
-        def transpose_w_out_block(blk):
-            grouped = stage.tile([P, PASSES, PACK * BLOCK], BF16, tag="x_grouped", align_bytes=64)
-            grouped_words = grouped[:].bitcast(F32).rearrange("p g (i u) -> p g i u", u=2)
-            for l in range(BLOCK // P):
-                words = wo_sb[:, blk * (BLOCK // P) + l, :].bitcast(F32)
-                flipped = psum.tile([P, PACK, P], F32, tag="first")
-                for b in range(PACK):
-                    nc.tensor.transpose(flipped[:, b, :], words[:, b * P : (b + 1) * P], ident[:])
-                nc.scalar.copy(
-                    out=grouped_words[:, :, l * P : (l + 1) * P, :],
-                    in_=flipped[:].rearrange("p (g u) i -> p g i u", u=2),
-                )
-            return grouped
-
-        wo_grouped = [transpose_w_out_block(blk) for blk in range(2)]
-
-        a_codes = keep.tile([P, PASSES, PASSES, K_PASS], U32, align_bytes=64)
-        a_scales = keep.tile([P, PASSES, PASSES, K_PASS], U8, align_bytes=64)
-
-        def regroup_a(g2, g):
+        def regroup_a(copy, g2, g):
             rows = ao_sb[:, g].rearrange("p u h c -> p (u h) c")[:, :, g2 * K_PASS : (g2 + 1) * K_PASS]
-            nc.vector.tensor_copy(
+            copy(
                 out=a_grouped[:, g2, g, :].rearrange("p (s c t) -> p s c t", s=PACK, t=PACK),
                 in_=rows.rearrange("p t (c s) -> p s c t", s=PACK),
             )
@@ -180,28 +156,67 @@ def tile_retentionmechanism_pc_kernel(
                 in_=a_grouped[:, g2, g, :],
             )
 
-        for g2 in range(PASSES):
-            for g in range(PASSES):
-                regroup_a(g2, g)
-            quantise_block(g2, wo_grouped[g2])
-            for g in range(PASSES):
-                quantise_a(g2, g)
+        x_codes = keep.tile([P, BLOCKS, SLICES, PASSES, P], U32, align_bytes=64)
+        x_scales = keep.tile([P, BLOCKS, SLICES, PASSES, P], U8, align_bytes=64)
+
+        def new_x_grouped():
+            x_grouped = stage.tile([P, SLICES, PASSES, P, PACK], BF16, tag="x_grouped", bufs=3, align_bytes=64)
+            return x_grouped
+
+        def transpose_w_out_slice(blk, l, grouped, bank_tag, copy):
+            words = wo_sb[:, blk * SLICES + l, :].bitcast(F32)
+            flipped = psum.tile([P, PACK, P], F32, tag=bank_tag, name="flipped")
+            for b in range(PACK):
+                nc.tensor.transpose(flipped[:, b, :], words[:, b * P : (b + 1) * P], ident[:])
+            copy(
+                out=grouped[:, l].rearrange("p g i t -> p g (i t)").bitcast(F32).rearrange("p g (i u) -> p g i u", u=2),
+                in_=flipped[:].rearrange("p (g u) i -> p g i u", u=2),
+            )
+
+        def quantise_x_slice(blk, l, grouped):
+            nc.vector.quantize_mx(
+                out=x_codes[:, blk, l].rearrange("p g c -> p (g c)").bitcast(FP8X4),
+                scales=x_scales[:, blk, l].rearrange("p g c -> p (g c)"),
+                in_=grouped[:, l].rearrange("p g i t -> p (g i t)"),
+            )
+
+        wo_grouped = new_x_grouped()
+        for l in range(SLICES):
+            transpose_w_out_slice(0, l, wo_grouped, "first", nc.scalar.copy)
+        for g in range(PASSES):
+            normalise_rows(g)
+            regroup_a(nc.vector.tensor_copy, 0, g)
+        quantise_x_slice(0, 0, wo_grouped)
+        for g in range(PASSES):
+            quantise_a(0, g)
+        for g in range(PASSES):
+            regroup_a(nc.scalar.copy, 1, g)
+        for l in range(1, SLICES):
+            quantise_x_slice(0, l, wo_grouped)
+        for g in range(PASSES):
+            quantise_a(1, g)
 
         gate = consts.tile([P, 2], F32)
         nc.vector.tensor_scalar(out=gate[:], in0=tao_sb[:], scalar1=-1.0, scalar2=None, op0=ALU.mult)
         nc.vector.tensor_tensor(out=gate[:], in0=gate[:], in1=tao_sb[:], op=ALU.max)
         nc.vector.tensor_scalar(out=gate[:], in0=gate[:], scalar1=1e-08, scalar2=1.0, op0=ALU.max, op1=ALU.min)
 
-        def regroup_v_block(blk):
-            cols = slice((blk - 2) * BLOCK, (blk - 1) * BLOCK)
-            grouped = stage.tile([P, PASSES, PACK * BLOCK], BF16, tag="x_grouped", align_bytes=64)
+        v_grouped = {}
+        for blk in (2, 3):
+            v_grouped[blk] = new_x_grouped()
             for g in range(PASSES):
-                rows = vq_sb[:, g].rearrange("p u h c -> p (u h) c")[:, :, cols]
-                nc.vector.tensor_copy(
-                    out=grouped[:, g, :].rearrange("p (c i t) -> p c t i", i=4, t=PACK),
-                    in_=rows.rearrange("p t (c i) -> p c t i", i=4),
+                rows = vq_sb[:, g].rearrange("p u h c -> p (u h) c")[:, :, (blk - 2) * BLOCK : (blk - 1) * BLOCK]
+                nc.gpsimd.tensor_scalar(
+                    out=v_grouped[blk][:, :, g, :, :], in0=rows.rearrange("p t (l c) -> p l c t", l=SLICES),
+                    scalar1=1.0, scalar2=0.0, op0=ALU.mult, op1=ALU.add,
                 )
-            quantise_block(blk, grouped)
+
+        def quantise_v_block(blk):
+            nc.vector.quantize_mx(
+                out=x_codes[:, blk].rearrange("p l g c -> p (l g c)").bitcast(FP8X4),
+                scales=x_scales[:, blk].rearrange("p l g c -> p (l g c)"),
+                in_=v_grouped[blk][:].rearrange("p l g c t -> p (l g c t)"),
+            )
 
         z2 = keep.tile([P, ROW_TILES, E], F32)
         z_of = {1: z2}
@@ -216,12 +231,11 @@ def tile_retentionmechanism_pc_kernel(
         n_scales = {}
 
         def first_product_bank(k):
-            blk, g2, cb = k // BANKS, (k % BANKS) // (BLOCK // P), k % (BLOCK // P)
+            blk, g2, cb = k // BANKS, (k % BANKS) // SLICES, k % SLICES
             if k % BANKS == 0:
                 n_grouped[blk] = stage.tile([P, PASSES, BLOCK, PACK], BF16, tag="n_grouped", name="n_grouped", align_bytes=64)
                 n_codes[blk] = stage.tile([P, PASSES, BLOCK], U32, tag="n_codes", name="n_codes", bufs=3, align_bytes=64)
                 n_scales[blk] = stage.tile([P, PASSES, BLOCK], U8, tag="n_scales", name="n_scales", bufs=3, align_bytes=64)
-            cols = slice(cb * P, (cb + 1) * P)
             bank = psum.tile([P, PACK, P], F32, tag="first")
             for s in range(PACK):
                 for g in range(PASSES):
@@ -229,38 +243,41 @@ def tile_retentionmechanism_pc_kernel(
                         out=bank[:, s, :],
                         lhsT=a_codes[:, g2, g, s * P : (s + 1) * P].bitcast(FP8X4),
                         lhsT_scale=a_scales[:, g2, g, s * P : (s + 1) * P],
-                        rhs=x_codes[:, blk, g, cols].bitcast(FP8X4),
-                        rhs_scale=x_scales[:, blk, g, cols],
+                        rhs=x_codes[:, blk, cb, g, :].bitcast(FP8X4),
+                        rhs_scale=x_scales[:, blk, cb, g, :],
                         start=(g == 0),
                         stop=(g == PASSES - 1),
                     )
             nc.scalar.activation(
-                out=n_grouped[blk][:, g2, cols, :], in_=bank[:].rearrange("p s c -> p c s"), func=ACT.Silu
+                out=n_grouped[blk][:, g2, cb * P : (cb + 1) * P, :], in_=bank[:].rearrange("p s c -> p c s"), func=ACT.Silu
             )
-            if cb == BLOCK // P - 1:
+            if cb == SLICES - 1:
                 nc.vector.quantize_mx(
                     out=n_codes[blk][:, g2, :].bitcast(FP8X4), scales=n_scales[blk][:, g2, :],
                     in_=n_grouped[blk][:, g2].rearrange("p c s -> p (c s)"),
                 )
 
+        def place_of_bank(k):
+            blk, b = k // BANKS, k % BANKS
+            if blk < 2:
+                return 1, blk * SLICES + b // 2, slice((b % 2) * BLOCK, (b % 2 + 1) * BLOCK)
+            return 0, b, slice((blk - 2) * BLOCK, (blk - 1) * BLOCK)
+
         def second_product_bank(k):
             blk, b = k // BANKS, k % BANKS
-            o = 1 if blk < 2 else 0
+            o, r, cols = place_of_bank(k)
             bank = psum.tile([P, BLOCK], F32, tag="second")
-            if o == 1:
-                r, cols = blk * (BLOCK // P) + b // 2, slice((b % 2) * BLOCK, (b % 2 + 1) * BLOCK)
-                inner = slice((b // 2) * P, (b // 2 + 1) * P)
-                for g2 in range(PASSES):
+            for g2 in range(PASSES):
+                if o == 1:
+                    inner = slice((b // 2) * P, (b // 2 + 1) * P)
                     nc.tensor.matmul_mx(
                         out=bank[:],
                         lhsT=n_codes[blk][:, g2, inner].bitcast(FP8X4), lhsT_scale=n_scales[blk][:, g2, inner],
                         rhs=w_codes[:, g2, cols].bitcast(FP8X4), rhs_scale=w_scales[:, g2, cols],
                         start=(g2 == 0), stop=(g2 == PASSES - 1),
                     )
-            else:
-                r, cols = b, slice((blk - 2) * BLOCK, (blk - 1) * BLOCK)
-                inner = slice(b * P, (b + 1) * P)
-                for g2 in range(PASSES):
+                else:
+                    inner = slice(r * P, (r + 1) * P)
                     nc.tensor.matmul_mx(
                         out=bank[:],
                         lhsT=w_codes[:, g2, inner].bitcast(FP8X4), lhsT_scale=w_scales[:, g2, inner],
@@ -269,18 +286,24 @@ def tile_retentionmechanism_pc_kernel(
                     )
             if k == 2 * BANKS:
                 z_of[0] = keep.tile([P, ROW_TILES, E], F32, tag="big", name="z1", align_bytes=64)
-            z = z_of[o]
             n_th = k % (2 * BANKS)
             nc.vector.scalar_tensor_tensor(
-                out=z[:, r, cols], in0=bank[:], scalar=1.0, in1=weight_of[o][:, r, cols],
+                out=z_of[o][:, r, cols], in0=bank[:], scalar=1.0, in1=weight_of[o][:, r, cols],
                 op0=ALU.mult, op1=ALU.add, accum_out=z_sum[o][:, n_th : n_th + 1],
             )
-            if b % 2 == 1:
-                done = z[:, r, :] if o == 1 else z[:, r - 1 : r + 1, cols]
-                sq_s = stage.tile([P, 2 * BLOCK], BF16, tag="sq_s", bufs=3)
-                sq_view = sq_s[:] if o == 1 else sq_s[:].rearrange("p (a c) -> p a c", a=2)
+
+        def square_two_banks(k):
+            o, r, cols = place_of_bank(k)
+            n_th = (k % (2 * BANKS)) // 2
+            sq_s = stage.tile([P, 2 * BLOCK], BF16, tag="sq_s", bufs=3)
+            if o == 1:
                 nc.scalar.activation(
-                    out=sq_view, in_=done, func=ACT.Square, accum_out=z_sumsq[o][:, n_th // 2 : n_th // 2 + 1]
+                    out=sq_s[:], in_=z_of[o][:, r, :], func=ACT.Square, accum_out=z_sumsq[o][:, n_th : n_th + 1]
+                )
+            else:
+                nc.scalar.activation(
+                    out=sq_s[:].rearrange("p (a c) -> p a c", a=2), in_=z_of[o][:, r - 1 : r + 1, cols], func=ACT.Square,
+                    accum_out=z_sumsq[o][:, n_th : n_th + 1],
                 )
 
         stats = {}
@@ -288,14 +311,16 @@ def tile_retentionmechanism_pc_kernel(
         work_of = {}
         std_of = {}
 
-        def sum_over_partitions(o):
+        def sum_along_free_axis(o):
             stats[o] = consts.tile([P, 2], F32, name="stats%d" % o)
             nc.vector.tensor_reduce(out=stats[o][:, 0:1], in_=z_sum[o][:], axis=AXIS.X, op=ALU.add)
             nc.vector.tensor_reduce(out=stats[o][:, 1:2], in_=z_sumsq[o][:], axis=AXIS.X, op=ALU.add)
+
+        def sum_over_partitions(o):
             totals[o] = psum.tile([P, BLOCK], F32, tag="second", name="totals")
             nc.tensor.matmul(out=totals[o][:, 0:2], lhsT=ones[:], rhs=stats[o][:], start=True, stop=True)
 
-        def variance(o):
+        def standard_deviation(o):
             work = consts.tile([P, 8], F32, name="work%d" % o)
             work_of[o] = work
             nc.vector.tensor_copy(out=work[:, 0:2], in_=totals[o][:, 0:2])
@@ -309,7 +334,7 @@ def tile_retentionmechanism_pc_kernel(
             std_of[o] = consts.tile([P, 1], F32, name="std%d" % o)
             nc.gpsimd.tensor_tensor(out=std_of[o][:], in0=work[:, 4:5], in1=half[:], op=ALU.pow)
 
-        def scale_and_store(o, engine, out_dram):
+        def scale_and_store(o, engines, out_dram):
             work = work_of[o]
             nc.vector.tensor_scalar(out=work[:, 5:6], in0=std_of[o][:], scalar1=EPS_STD, scalar2=None, op0=ALU.add)
             nc.vector.reciprocal(out=work[:, 6:7], in_=work[:, 5:6])
@@ -318,27 +343,43 @@ def tile_retentionmechanism_pc_kernel(
             )
             rows = by_row_tile(out_dram)
             for r in range(ROW_TILES):
-                engine.tensor_scalar(
-                    out=z_of[o][:, r, :], in0=z_of[o][:, r, :], scalar1=work[:, 7:8], scalar2=1.0, op0=ALU.mult, op1=ALU.mult
-                )
+                engine = engines[r % len(engines)]
+                if engine is nc.scalar:
+                    nc.scalar.activation(out=z_of[o][:, r, :], in_=z_of[o][:, r, :], func=ACT.Copy, scale=work[:, 7:8])
+                else:
+                    engine.tensor_scalar(
+                        out=z_of[o][:, r, :], in0=z_of[o][:, r, :], scalar1=work[:, 7:8], scalar2=1.0, op0=ALU.mult, op1=ALU.mult
+                    )
                 nc.sync.dma_start(out=rows[:, r, :], in_=z_of[o][:, r, :])
 
         total_banks = BLOCKS * BANKS
         behind = BANKS + LAG
-        out2_done = 2 * BANKS - 1 + behind + STATS_LAG
-        for step in range(total_banks + behind):
+        out2_squared = 2 * BANKS - 1 + behind + SQUARE_LAG
+        for step in range(total_banks + behind + SQUARE_LAG):
+            to_square = step - behind - SQUARE_LAG
+            if to_square >= 0 and to_square % 2 == 1:
+                square_two_banks(to_square)
+            if step == out2_squared:
+                sum_along_free_axis(1)
+            if step == out2_squared + 1:
+                sum_over_partitions(1)
+            if step == out2_squared + 2:
+                standard_deviation(1)
+            if step == out2_squared + 3:
+                scale_and_store(1, [nc.gpsimd], out_1)
+            if step == LAG:
+                wo_grouped = new_x_grouped()
+                for l in range(SLICES):
+                    transpose_w_out_slice(1, l, wo_grouped, "second", nc.vector.tensor_copy)
+                for l in range(SLICES):
+                    quantise_x_slice(1, l, wo_grouped)
             if step in (BANKS, 2 * BANKS):
-                regroup_v_block(step // BANKS + 1)
+                quantise_v_block(step // BANKS + 1)
             if step < total_banks:
                 first_product_bank(step)
-            if step >= behind:
+            if behind <= step < total_banks + behind:
                 second_product_bank(step - behind)
-            if step == out2_done:
-                sum_over_partitions(1)
-            if step == out2_done + 1:
-                variance(1)
-            if step == out2_done + 2:
-                scale_and_store(1, nc.gpsimd, out_1)
+        sum_along_free_axis(0)
         sum_over_partitions(0)
-        variance(0)
-        scale_and_store(0, nc.vector, out1_dram)
+        standard_deviation(0)
+        scale_and_store(0, [nc.vector, nc.scalar], out1_dram)

@@ -202,14 +202,15 @@ def tile_retentionmechanism_pc_kernel(
         nc.vector.tensor_scalar(out=gate[:], in0=gate[:], scalar1=1e-08, scalar2=1.0, op0=ALU.max, op1=ALU.min)
 
         v_grouped = {}
-        for blk in (2, 3):
-            v_grouped[blk] = new_x_grouped()
-            for g in range(PASSES):
-                rows = vq_sb[:, g].rearrange("p u h c -> p (u h) c")[:, :, (blk - 2) * BLOCK : (blk - 1) * BLOCK]
-                nc.gpsimd.tensor_scalar(
-                    out=v_grouped[blk][:, :, g, :, :], in0=rows.rearrange("p t (l c) -> p l c t", l=SLICES),
-                    scalar1=1.0, scalar2=0.0, op0=ALU.mult, op1=ALU.add,
-                )
+
+        def regroup_v(blk, g):
+            if g == 0:
+                v_grouped[blk] = new_x_grouped()
+            rows = vq_sb[:, g].rearrange("p u h c -> p (u h) c")[:, :, (blk - 2) * BLOCK : (blk - 1) * BLOCK]
+            nc.vector.tensor_copy(
+                out=v_grouped[blk][:, :, g, :, :].rearrange("p l (c i) t -> p l c t i", i=4),
+                in_=rows.rearrange("p t (l c i) -> p l c t i", l=SLICES, i=4),
+            )
 
         def quantise_v_block(blk):
             nc.vector.quantize_mx(
@@ -373,8 +374,12 @@ def tile_retentionmechanism_pc_kernel(
                     transpose_w_out_slice(1, l, wo_grouped, "second", nc.vector.tensor_copy)
                 for l in range(SLICES):
                     quantise_x_slice(1, l, wo_grouped)
-            if step in (BANKS, 2 * BANKS):
-                quantise_v_block(step // BANKS + 1)
+            next_blk, within = step // BANKS + 1, step % BANKS
+            if next_blk in (2, 3):
+                if within in (2, 4):
+                    regroup_v(next_blk, within // 2 - 1)
+                if within == 6:
+                    quantise_v_block(next_blk)
             if step < total_banks:
                 first_product_bank(step)
             if behind <= step < total_banks + behind:

@@ -61,6 +61,8 @@ def tile_retentionmechanism_pc_kernel(
         make_identity(nc, ident[:])
         ones = consts.tile([P, P], F32)
         nc.gpsimd.memset(ones[:], 1.0)
+        ones_over_count = consts.tile([P, P], F32)
+        nc.gpsimd.memset(ones_over_count[:], 1.0 / COUNT)
         warm = consts.tile([P, 1], F32)
         nc.scalar.activation(out=warm[:], in_=half[:], func=ACT.Silu)
 
@@ -78,13 +80,22 @@ def tile_retentionmechanism_pc_kernel(
         wo_sb = keep.tile([P, ROW_TILES, E], BF16)
         wo_rows = by_row_tile(w_out)
 
-        def load_w_out_block(blk):
-            for r in range(blk * SLICES, (blk + 1) * SLICES, 2):
-                nc.sync.dma_start(out=wo_sb[:, r : r + 2, :], in_=wo_rows[:, r : r + 2, :])
-
-        load_w_out_block(0)
+        for r in range(0, ROW_TILES, 2):
+            nc.sync.dma_start(out=wo_sb[:, r : r + 2, :], in_=wo_rows[:, r : r + 2, :])
 
         w_codes = keep.tile([P, PASSES, E], U32, align_bytes=64)
+        for g2 in range(PASSES):
+            nc.sync.dma_start(
+                out=w_codes[:, g2, :].bitcast(I32),
+                in_=out_w_words[g2].rearrange("p n t -> p (n t)").bitcast(I32),
+            )
+
+        vq_sb = keep.tile([P, PASSES, 2, 2, E], BF16)
+        v_rows = by_word_order(v_dram)
+        for g in range(PASSES):
+            for u in range(2):
+                nc.sync.dma_start(out=vq_sb[:, g, u], in_=v_rows[g, u])
+
         w_scales = keep.tile([P, PASSES, E], U8, align_bytes=64)
         nc.vector.memset(w_scales[:].rearrange("p g n -> p (g n)").bitcast(I32), 0)
         for quad in range(4):
@@ -92,18 +103,6 @@ def tile_retentionmechanism_pc_kernel(
                 out=w_scales[32 * quad : 32 * quad + 4].bitcast(I32),
                 in_=out_w_scales[:, 4 * quad : 4 * quad + 4, :].rearrange("g r n -> r g n").bitcast(I32),
             )
-        for g2 in range(PASSES):
-            nc.sync.dma_start(
-                out=w_codes[:, g2, :].bitcast(I32),
-                in_=out_w_words[g2].rearrange("p n t -> p (n t)").bitcast(I32),
-            )
-        load_w_out_block(1)
-
-        vq_sb = keep.tile([P, PASSES, 2, 2, E], BF16)
-        v_rows = by_word_order(v_dram)
-        for g in range(PASSES):
-            for u in range(2):
-                nc.sync.dma_start(out=vq_sb[:, g, u], in_=v_rows[g, u])
         v_sb = keep.tile([P, ROW_TILES, E], BF16)
         v_tiles = by_row_tile(v_dram)
         for r in range(0, ROW_TILES, 2):
@@ -146,8 +145,8 @@ def tile_retentionmechanism_pc_kernel(
         def regroup_a(copy, g2, g):
             rows = ao_sb[:, g].rearrange("p u h c -> p (u h) c")[:, :, g2 * K_PASS : (g2 + 1) * K_PASS]
             copy(
-                out=a_grouped[:, g2, g, :].rearrange("p (s c t) -> p s c t", s=PACK, t=PACK),
-                in_=rows.rearrange("p t (c s) -> p s c t", s=PACK),
+                out=a_grouped[:, g2, g, :].rearrange("p (s c t) -> p c t s", s=PACK, t=PACK),
+                in_=rows.rearrange("p t (c s) -> p c t s", s=PACK),
             )
 
         def quantise_a(g2, g):
@@ -200,6 +199,8 @@ def tile_retentionmechanism_pc_kernel(
         nc.vector.tensor_scalar(out=gate[:], in0=tao_sb[:], scalar1=-1.0, scalar2=None, op0=ALU.mult)
         nc.vector.tensor_tensor(out=gate[:], in0=gate[:], in1=tao_sb[:], op=ALU.max)
         nc.vector.tensor_scalar(out=gate[:], in0=gate[:], scalar1=1e-08, scalar2=1.0, op0=ALU.max, op1=ALU.min)
+        gate_target = consts.tile([P, 2], F32)
+        nc.vector.tensor_scalar(out=gate_target[:], in0=gate[:], scalar1=TARGET_STD, scalar2=None, op0=ALU.mult)
 
         v_grouped = {}
 
@@ -222,11 +223,10 @@ def tile_retentionmechanism_pc_kernel(
         z2 = keep.tile([P, ROW_TILES, E], F32)
         z_of = {1: z2}
         weight_of = {0: v_sb, 1: wo_sb}
-        z_sum = {}
-        z_sumsq = {}
+        partial = {}
         for o in range(2):
-            z_sum[o] = consts.tile([P, 2 * BANKS], F32, name="z_sum%d" % o)
-            z_sumsq[o] = consts.tile([P, BANKS], F32, name="z_sumsq%d" % o)
+            partial[o] = consts.tile([P, 2, 2 * BANKS], F32, name="partial%d" % o)
+            nc.gpsimd.memset(partial[o][:], 0.0)
         n_grouped = {}
         n_codes = {}
         n_scales = {}
@@ -290,7 +290,7 @@ def tile_retentionmechanism_pc_kernel(
             n_th = k % (2 * BANKS)
             nc.vector.scalar_tensor_tensor(
                 out=z_of[o][:, r, cols], in0=bank[:], scalar=1.0, in1=weight_of[o][:, r, cols],
-                op0=ALU.mult, op1=ALU.add, accum_out=z_sum[o][:, n_th : n_th + 1],
+                op0=ALU.mult, op1=ALU.add, accum_out=partial[o][:, 0, n_th : n_th + 1],
             )
 
         def square_two_banks(k):
@@ -299,59 +299,50 @@ def tile_retentionmechanism_pc_kernel(
             sq_s = stage.tile([P, 2 * BLOCK], BF16, tag="sq_s", bufs=3)
             if o == 1:
                 nc.scalar.activation(
-                    out=sq_s[:], in_=z_of[o][:, r, :], func=ACT.Square, accum_out=z_sumsq[o][:, n_th : n_th + 1]
+                    out=sq_s[:], in_=z_of[o][:, r, :], func=ACT.Square, accum_out=partial[o][:, 1, n_th : n_th + 1]
                 )
             else:
                 nc.scalar.activation(
                     out=sq_s[:].rearrange("p (a c) -> p a c", a=2), in_=z_of[o][:, r - 1 : r + 1, cols], func=ACT.Square,
-                    accum_out=z_sumsq[o][:, n_th : n_th + 1],
+                    accum_out=partial[o][:, 1, n_th : n_th + 1],
                 )
 
-        stats = {}
         totals = {}
         work_of = {}
         std_of = {}
 
-        def sum_along_free_axis(o):
-            stats[o] = consts.tile([P, 2], F32, name="stats%d" % o)
-            nc.vector.tensor_reduce(out=stats[o][:, 0:1], in_=z_sum[o][:], axis=AXIS.X, op=ALU.add)
-            nc.vector.tensor_reduce(out=stats[o][:, 1:2], in_=z_sumsq[o][:], axis=AXIS.X, op=ALU.add)
-
         def sum_over_partitions(o):
-            totals[o] = psum.tile([P, BLOCK], F32, tag="second", name="totals")
-            nc.tensor.matmul(out=totals[o][:, 0:2], lhsT=ones[:], rhs=stats[o][:], start=True, stop=True)
+            totals[o] = psum.tile([P, 3, 2 * BANKS], F32, tag="second", name="totals")
+            nc.tensor.matmul(
+                out=totals[o][:, 0:2, :].rearrange("p a k -> p (a k)"), lhsT=ones[:],
+                rhs=partial[o][:].rearrange("p a k -> p (a k)"), start=True, stop=True,
+            )
+            nc.tensor.matmul(out=totals[o][:, 2, :], lhsT=ones_over_count[:], rhs=partial[o][:, 0, :], start=True, stop=True)
 
         def standard_deviation(o):
             work = consts.tile([P, 8], F32, name="work%d" % o)
             work_of[o] = work
-            nc.vector.tensor_copy(out=work[:, 0:2], in_=totals[o][:, 0:2])
-            nc.vector.tensor_scalar(out=work[:, 2:3], in0=work[:, 0:1], scalar1=-1.0 / COUNT, scalar2=None, op0=ALU.mult)
+            nc.vector.tensor_reduce(out=work[:, 0:3], in_=totals[o][:], axis=AXIS.X, op=ALU.add)
             nc.vector.scalar_tensor_tensor(
-                out=work[:, 3:4], in0=work[:, 0:1], scalar=work[:, 2:3], in1=work[:, 1:2], op0=ALU.mult, op1=ALU.add
+                out=work[:, 3:4], in0=work[:, 0:1], scalar=work[:, 2:3], in1=work[:, 1:2], op0=ALU.mult, op1=ALU.subtract
             )
             nc.vector.tensor_scalar(
-                out=work[:, 4:5], in0=work[:, 3:4], scalar1=1.0 / (COUNT - 1), scalar2=0.0, op0=ALU.mult, op1=ALU.max
+                out=work[:, 4:5], in0=work[:, 3:4], scalar1=-1.0 / (COUNT - 1), scalar2=0.0, op0=ALU.mult, op1=ALU.max
             )
             std_of[o] = consts.tile([P, 1], F32, name="std%d" % o)
             nc.gpsimd.tensor_tensor(out=std_of[o][:], in0=work[:, 4:5], in1=half[:], op=ALU.pow)
 
-        def scale_and_store(o, engines, out_dram):
+        def scale_and_store(o, engine, tiles_at_once, out_dram):
             work = work_of[o]
             nc.vector.tensor_scalar(out=work[:, 5:6], in0=std_of[o][:], scalar1=EPS_STD, scalar2=None, op0=ALU.add)
             nc.vector.reciprocal(out=work[:, 6:7], in_=work[:, 5:6])
-            nc.vector.tensor_scalar(
-                out=work[:, 7:8], in0=work[:, 6:7], scalar1=gate[:, o : o + 1], scalar2=TARGET_STD, op0=ALU.mult, op1=ALU.mult
-            )
             rows = by_row_tile(out_dram)
-            for r in range(ROW_TILES):
-                engine = engines[r % len(engines)]
-                if engine is nc.scalar:
-                    nc.scalar.activation(out=z_of[o][:, r, :], in_=z_of[o][:, r, :], func=ACT.Copy, scale=work[:, 7:8])
-                else:
-                    engine.tensor_scalar(
-                        out=z_of[o][:, r, :], in0=z_of[o][:, r, :], scalar1=work[:, 7:8], scalar2=1.0, op0=ALU.mult, op1=ALU.mult
-                    )
-                nc.sync.dma_start(out=rows[:, r, :], in_=z_of[o][:, r, :])
+            for r in range(0, ROW_TILES, tiles_at_once):
+                piece = z_of[o][:, r : r + tiles_at_once, :]
+                engine.tensor_scalar(
+                    out=piece, in0=piece, scalar1=work[:, 6:7], scalar2=gate_target[:, o : o + 1], op0=ALU.mult, op1=ALU.mult
+                )
+                nc.sync.dma_start(out=rows[:, r : r + tiles_at_once, :], in_=piece)
 
         total_banks = BLOCKS * BANKS
         behind = BANKS + LAG
@@ -360,14 +351,12 @@ def tile_retentionmechanism_pc_kernel(
             to_square = step - behind - SQUARE_LAG
             if to_square >= 0 and to_square % 2 == 1:
                 square_two_banks(to_square)
-            if step == out2_squared:
-                sum_along_free_axis(1)
             if step == out2_squared + 1:
                 sum_over_partitions(1)
             if step == out2_squared + 2:
                 standard_deviation(1)
             if step == out2_squared + 3:
-                scale_and_store(1, [nc.gpsimd], out_1)
+                scale_and_store(1, nc.gpsimd, 2, out_1)
             if step == LAG:
                 wo_grouped = new_x_grouped()
                 for l in range(SLICES):
@@ -384,7 +373,6 @@ def tile_retentionmechanism_pc_kernel(
                 first_product_bank(step)
             if behind <= step < total_banks + behind:
                 second_product_bank(step - behind)
-        sum_along_free_axis(0)
         sum_over_partitions(0)
         standard_deviation(0)
-        scale_and_store(0, [nc.vector, nc.scalar], out1_dram)
+        scale_and_store(0, nc.vector, 1, out1_dram)

@@ -27,6 +27,8 @@ EPS_RMS = 1.1920929e-07
 EPS_STD = 1e-08
 COUNT = E * E
 TARGET_STD = 512.0 ** -0.5
+REGROUP_STEPS = {8: (2, 0), 10: (2, 1), 14: (3, 0), 17: (3, 1)}
+QUANTISE_STEPS = {12: 2, 20: 3}
 LAG = 2
 SQUARE_LAG = 3
 
@@ -83,11 +85,12 @@ def tile_retentionmechanism_pc_kernel(
         for r in range(0, ROW_TILES, 2):
             nc.sync.dma_start(out=wo_sb[:, r : r + 2, :], in_=wo_rows[:, r : r + 2, :])
 
-        w_codes = keep.tile([P, PASSES, E], U32, align_bytes=64)
-        for g2 in range(PASSES):
+        w_scales = keep.tile([P, PASSES, E], U8, align_bytes=64)
+        nc.vector.memset(w_scales[:].rearrange("p g n -> p (g n)").bitcast(I32), 0)
+        for quad in range(4):
             nc.sync.dma_start(
-                out=w_codes[:, g2, :].bitcast(I32),
-                in_=out_w_words[g2].rearrange("p n t -> p (n t)").bitcast(I32),
+                out=w_scales[32 * quad : 32 * quad + 4].bitcast(I32),
+                in_=out_w_scales[:, 4 * quad : 4 * quad + 4, :].rearrange("g r n -> r g n").bitcast(I32),
             )
 
         vq_sb = keep.tile([P, PASSES, 2, 2, E], BF16)
@@ -96,13 +99,13 @@ def tile_retentionmechanism_pc_kernel(
             for u in range(2):
                 nc.sync.dma_start(out=vq_sb[:, g, u], in_=v_rows[g, u])
 
-        w_scales = keep.tile([P, PASSES, E], U8, align_bytes=64)
-        nc.vector.memset(w_scales[:].rearrange("p g n -> p (g n)").bitcast(I32), 0)
-        for quad in range(4):
+        w_codes = keep.tile([P, PASSES, E], U32, align_bytes=64)
+        for g2 in range(PASSES):
             nc.sync.dma_start(
-                out=w_scales[32 * quad : 32 * quad + 4].bitcast(I32),
-                in_=out_w_scales[:, 4 * quad : 4 * quad + 4, :].rearrange("g r n -> r g n").bitcast(I32),
+                out=w_codes[:, g2, :].bitcast(I32),
+                in_=out_w_words[g2].rearrange("p n t -> p (n t)").bitcast(I32),
             )
+
         v_sb = keep.tile([P, ROW_TILES, E], BF16)
         v_tiles = by_row_tile(v_dram)
         for r in range(0, ROW_TILES, 2):
@@ -162,11 +165,14 @@ def tile_retentionmechanism_pc_kernel(
             x_grouped = stage.tile([P, SLICES, PASSES, P, PACK], BF16, tag="x_grouped", bufs=3, align_bytes=64)
             return x_grouped
 
-        def transpose_w_out_slice(blk, l, grouped, bank_tag, copy):
+        def transpose_w_out_slice(blk, l, bank_tag):
             words = wo_sb[:, blk * SLICES + l, :].bitcast(F32)
             flipped = psum.tile([P, PACK, P], F32, tag=bank_tag, name="flipped")
             for b in range(PACK):
                 nc.tensor.transpose(flipped[:, b, :], words[:, b * P : (b + 1) * P], ident[:])
+            return flipped
+
+        def empty_transposes(copy, flipped, grouped, l):
             copy(
                 out=grouped[:, l].rearrange("p g i t -> p g (i t)").bitcast(F32).rearrange("p g (i u) -> p g i u", u=2),
                 in_=flipped[:].rearrange("p (g u) i -> p g i u", u=2),
@@ -181,7 +187,10 @@ def tile_retentionmechanism_pc_kernel(
 
         wo_grouped = new_x_grouped()
         for l in range(SLICES):
-            transpose_w_out_slice(0, l, wo_grouped, "first", nc.scalar.copy)
+            empty_transposes(nc.scalar.copy, transpose_w_out_slice(0, l, "first"), wo_grouped, l)
+        next_flipped = {}
+        for l in range(SLICES):
+            next_flipped[l] = transpose_w_out_slice(1, l, "second")
         for g in range(PASSES):
             normalise_rows(g)
             regroup_a(nc.vector.tensor_copy, 0, g)
@@ -252,11 +261,13 @@ def tile_retentionmechanism_pc_kernel(
             nc.scalar.activation(
                 out=n_grouped[blk][:, g2, cb * P : (cb + 1) * P, :], in_=bank[:].rearrange("p s c -> p c s"), func=ACT.Silu
             )
-            if cb == SLICES - 1:
-                nc.vector.quantize_mx(
-                    out=n_codes[blk][:, g2, :].bitcast(FP8X4), scales=n_scales[blk][:, g2, :],
-                    in_=n_grouped[blk][:, g2].rearrange("p c s -> p (c s)"),
-                )
+
+        def quantise_n(k):
+            blk, g2 = k // BANKS, (k % BANKS) // SLICES
+            nc.vector.quantize_mx(
+                out=n_codes[blk][:, g2, :].bitcast(FP8X4), scales=n_scales[blk][:, g2, :],
+                in_=n_grouped[blk][:, g2].rearrange("p c s -> p (c s)"),
+            )
 
         def place_of_bank(k):
             blk, b = k // BANKS, k % BANKS
@@ -356,23 +367,23 @@ def tile_retentionmechanism_pc_kernel(
             if step == out2_squared + 2:
                 standard_deviation(1)
             if step == out2_squared + 3:
-                scale_and_store(1, nc.gpsimd, 2, out_1)
+                scale_and_store(1, nc.gpsimd, 1, out_1)
             if step == LAG:
                 wo_grouped = new_x_grouped()
                 for l in range(SLICES):
-                    transpose_w_out_slice(1, l, wo_grouped, "second", nc.vector.tensor_copy)
+                    empty_transposes(nc.vector.tensor_copy, next_flipped[l], wo_grouped, l)
                 for l in range(SLICES):
                     quantise_x_slice(1, l, wo_grouped)
-            next_blk, within = step // BANKS + 1, step % BANKS
-            if next_blk in (2, 3):
-                if within in (2, 4):
-                    regroup_v(next_blk, within // 2 - 1)
-                if within == 6:
-                    quantise_v_block(next_blk)
+            if step in REGROUP_STEPS:
+                regroup_v(*REGROUP_STEPS[step])
+            if step in QUANTISE_STEPS:
+                quantise_v_block(QUANTISE_STEPS[step])
             if step < total_banks:
                 first_product_bank(step)
             if behind <= step < total_banks + behind:
                 second_product_bank(step - behind)
+            if step < total_banks and step % SLICES == SLICES - 1:
+                quantise_n(step)
         sum_over_partitions(0)
         standard_deviation(0)
         scale_and_store(0, nc.vector, 1, out1_dram)

@@ -29,6 +29,7 @@ COUNT = E * E
 TARGET_STD = 512.0 ** -0.5
 REGROUP_STEPS = {8: (2, 0), 10: (2, 1), 14: (3, 0), 17: (3, 1)}
 QUANTISE_STEPS = {12: 2, 20: 3}
+G_TILES = 7
 LAG = 2
 SQUARE_LAG = 3
 
@@ -63,8 +64,10 @@ def tile_retentionmechanism_pc_kernel(
         make_identity(nc, ident[:])
         ones = consts.tile([P, P], F32)
         nc.gpsimd.memset(ones[:], 1.0)
-        ones_over_count = consts.tile([P, P], F32)
-        nc.gpsimd.memset(ones_over_count[:], 1.0 / COUNT)
+        square_weight = consts.tile([P, P], F32)
+        nc.gpsimd.memset(square_weight[:], 1.0 / (COUNT - 1))
+        mean_weight = consts.tile([P, P], F32)
+        nc.gpsimd.memset(mean_weight[:], -1.0 / (COUNT * (COUNT - 1)))
         warm = consts.tile([P, 1], F32)
         nc.scalar.activation(out=warm[:], in_=half[:], func=ACT.Silu)
 
@@ -233,9 +236,11 @@ def tile_retentionmechanism_pc_kernel(
         z_of = {1: z2}
         weight_of = {0: v_sb, 1: wo_sb}
         partial = {}
+        last_square = {}
         for o in range(2):
             partial[o] = consts.tile([P, 2, 2 * BANKS], F32, name="partial%d" % o)
             nc.gpsimd.memset(partial[o][:], 0.0)
+            last_square[o] = consts.tile([P, 1], F32, name="last_square%d" % o)
         n_grouped = {}
         n_codes = {}
         n_scales = {}
@@ -307,6 +312,15 @@ def tile_retentionmechanism_pc_kernel(
         def square_two_banks(k):
             o, r, cols = place_of_bank(k)
             n_th = (k % (2 * BANKS)) // 2
+            if n_th == BANKS - 1:
+                for col, bank in ((0, k - 1), (1, k)):
+                    o, r, cols = place_of_bank(bank)
+                    sq_s = stage.tile([P, 2 * BLOCK], BF16, tag="sq_s", bufs=3)
+                    nc.scalar.activation(
+                        out=sq_s[:, 0:BLOCK], in_=z_of[o][:, r, cols], func=ACT.Square,
+                        accum_out=last_square[o][:] if col else partial[o][:, 1, n_th : n_th + 1],
+                    )
+                return
             sq_s = stage.tile([P, 2 * BLOCK], BF16, tag="sq_s", bufs=3)
             if o == 1:
                 nc.scalar.activation(
@@ -320,40 +334,47 @@ def tile_retentionmechanism_pc_kernel(
 
         totals = {}
         work_of = {}
-        std_of = {}
+
+        def sum_within_partitions(o):
+            work_of[o] = consts.tile([P, 8], F32, name="work%d" % o)
+            nc.vector.tensor_reduce(out=work_of[o][:, 0:2], in_=partial[o][:], axis=AXIS.X, op=ALU.add)
 
         def sum_over_partitions(o):
-            totals[o] = psum.tile([P, 3, 2 * BANKS], F32, tag="second", name="totals")
-            nc.tensor.matmul(
-                out=totals[o][:, 0:2, :].rearrange("p a k -> p (a k)"), lhsT=ones[:],
-                rhs=partial[o][:].rearrange("p a k -> p (a k)"), start=True, stop=True,
-            )
-            nc.tensor.matmul(out=totals[o][:, 2, :], lhsT=ones_over_count[:], rhs=partial[o][:, 0, :], start=True, stop=True)
+            work = work_of[o]
+            sums = psum.tile([P, 2], F32, tag="second", name="sums")
+            nc.tensor.matmul(out=sums[:, 0:1], lhsT=ones[:], rhs=work[:, 0:1], start=True, stop=True)
+            nc.tensor.matmul(out=sums[:, 1:2], lhsT=mean_weight[:], rhs=work[:, 0:1], start=True, stop=True)
+            squares = psum.tile([P, 1], F32, tag="second", name="squares")
+            nc.tensor.matmul(out=squares[:], lhsT=square_weight[:], rhs=work[:, 1:2], start=True, stop=False)
+            nc.tensor.matmul(out=squares[:], lhsT=square_weight[:], rhs=last_square[o][:], start=False, stop=True)
+            totals[o] = sums, squares
 
         def standard_deviation(o):
-            work = consts.tile([P, 8], F32, name="work%d" % o)
-            work_of[o] = work
-            nc.vector.tensor_reduce(out=work[:, 0:3], in_=totals[o][:], axis=AXIS.X, op=ALU.add)
-            nc.vector.scalar_tensor_tensor(
-                out=work[:, 3:4], in0=work[:, 0:1], scalar=work[:, 2:3], in1=work[:, 1:2], op0=ALU.mult, op1=ALU.subtract
-            )
-            nc.vector.tensor_scalar(
-                out=work[:, 4:5], in0=work[:, 3:4], scalar1=-1.0 / (COUNT - 1), scalar2=0.0, op0=ALU.mult, op1=ALU.max
-            )
-            std_of[o] = consts.tile([P, 1], F32, name="std%d" % o)
-            nc.gpsimd.tensor_tensor(out=std_of[o][:], in0=work[:, 4:5], in1=half[:], op=ALU.pow)
-
-        def scale_and_store(o, engine, tiles_at_once, out_dram):
             work = work_of[o]
-            nc.vector.tensor_scalar(out=work[:, 5:6], in0=std_of[o][:], scalar1=EPS_STD, scalar2=None, op0=ALU.add)
-            nc.vector.reciprocal(out=work[:, 6:7], in_=work[:, 5:6])
+            sums, squares = totals[o]
+            nc.vector.tensor_copy(out=work[:, 2:4], in_=sums[:])
+            nc.vector.tensor_tensor(out=work[:, 4:5], in0=work[:, 2:3], in1=work[:, 3:4], op=ALU.mult)
+            nc.vector.tensor_scalar(
+                out=work[:, 5:6], in0=squares[:], scalar1=work[:, 4:5], scalar2=0.0, op0=ALU.add, op1=ALU.max
+            )
+            std = consts.tile([P, 1], F32, name="std%d" % o)
+            nc.gpsimd.tensor_tensor(out=std[:], in0=work[:, 5:6], in1=half[:], op=ALU.pow)
+            return std
+
+        def factor(o, std):
+            work = work_of[o]
+            nc.vector.tensor_scalar(out=work[:, 6:7], in0=std[:], scalar1=EPS_STD, scalar2=None, op0=ALU.add)
+            nc.vector.reciprocal(out=work[:, 7:8], in_=work[:, 6:7])
+
+        def scale_and_store(o, engine, tiles, out_dram):
             rows = by_row_tile(out_dram)
-            for r in range(0, ROW_TILES, tiles_at_once):
-                piece = z_of[o][:, r : r + tiles_at_once, :]
+            for r in tiles:
+                piece = z_of[o][:, r, :]
                 engine.tensor_scalar(
-                    out=piece, in0=piece, scalar1=work[:, 6:7], scalar2=gate_target[:, o : o + 1], op0=ALU.mult, op1=ALU.mult
+                    out=piece, in0=piece, scalar1=work_of[o][:, 7:8], scalar2=gate_target[:, o : o + 1],
+                    op0=ALU.mult, op1=ALU.mult,
                 )
-                nc.sync.dma_start(out=rows[:, r : r + tiles_at_once, :], in_=piece)
+                nc.sync.dma_start(out=rows[:, r, :], in_=piece)
 
         total_banks = BLOCKS * BANKS
         behind = BANKS + LAG
@@ -363,11 +384,9 @@ def tile_retentionmechanism_pc_kernel(
             if to_square >= 0 and to_square % 2 == 1:
                 square_two_banks(to_square)
             if step == out2_squared + 1:
-                sum_over_partitions(1)
+                sum_within_partitions(1)
             if step == out2_squared + 2:
-                standard_deviation(1)
-            if step == out2_squared + 3:
-                scale_and_store(1, nc.gpsimd, 1, out_1)
+                std = standard_deviation(1)
             if step == LAG:
                 wo_grouped = new_x_grouped()
                 for l in range(SLICES):
@@ -384,6 +403,13 @@ def tile_retentionmechanism_pc_kernel(
                 second_product_bank(step - behind)
             if step < total_banks and step % SLICES == SLICES - 1:
                 quantise_n(step)
+            if step == out2_squared + 1:
+                sum_over_partitions(1)
+            if step == out2_squared + 2:
+                factor(1, std)
+                scale_and_store(1, nc.gpsimd, range(0, G_TILES), out_1)
+        scale_and_store(1, nc.vector, range(G_TILES, ROW_TILES), out_1)
+        sum_within_partitions(0)
         sum_over_partitions(0)
-        standard_deviation(0)
-        scale_and_store(0, nc.vector, 1, out1_dram)
+        factor(0, standard_deviation(0))
+        scale_and_store(0, nc.vector, range(ROW_TILES), out1_dram)

@@ -29,7 +29,7 @@ COUNT = E * E
 TARGET_STD = 512.0 ** -0.5
 REGROUP_STEPS = {8: (2, 0), 10: (2, 1), 14: (3, 0), 17: (3, 1)}
 QUANTISE_STEPS = {12: 2, 20: 3}
-G_TILES = 7
+G_TILES = 5
 LAG = 2
 SQUARE_LAG = 3
 
@@ -62,12 +62,8 @@ def tile_retentionmechanism_pc_kernel(
         nc.gpsimd.memset(minus_half[:], -0.5)
         ident = consts.tile([P, P], F32)
         make_identity(nc, ident[:])
-        ones = consts.tile([P, P], F32)
-        nc.gpsimd.memset(ones[:], 1.0)
-        square_weight = consts.tile([P, P], F32)
-        nc.gpsimd.memset(square_weight[:], 1.0 / (COUNT - 1))
-        mean_weight = consts.tile([P, P], F32)
-        nc.gpsimd.memset(mean_weight[:], -1.0 / (COUNT * (COUNT - 1)))
+        over_divisor = consts.tile([P, P], F32)
+        nc.gpsimd.memset(over_divisor[:], 1.0 / (COUNT - 1))
         warm = consts.tile([P, 1], F32)
         nc.scalar.activation(out=warm[:], in_=half[:], func=ACT.Silu)
 
@@ -236,11 +232,11 @@ def tile_retentionmechanism_pc_kernel(
         z_of = {1: z2}
         weight_of = {0: v_sb, 1: wo_sb}
         partial = {}
-        last_square = {}
+        last_squares = {}
         for o in range(2):
             partial[o] = consts.tile([P, 2, 2 * BANKS], F32, name="partial%d" % o)
             nc.gpsimd.memset(partial[o][:], 0.0)
-            last_square[o] = consts.tile([P, 1], F32, name="last_square%d" % o)
+            last_squares[o] = consts.tile([P, 2], F32, name="last_squares%d" % o)
         n_grouped = {}
         n_codes = {}
         n_scales = {}
@@ -318,7 +314,7 @@ def tile_retentionmechanism_pc_kernel(
                     sq_s = stage.tile([P, 2 * BLOCK], BF16, tag="sq_s", bufs=3)
                     nc.scalar.activation(
                         out=sq_s[:, 0:BLOCK], in_=z_of[o][:, r, cols], func=ACT.Square,
-                        accum_out=last_square[o][:] if col else partial[o][:, 1, n_th : n_th + 1],
+                        accum_out=last_squares[o][:, col : col + 1],
                     )
                 return
             sq_s = stage.tile([P, 2 * BLOCK], BF16, tag="sq_s", bufs=3)
@@ -340,20 +336,21 @@ def tile_retentionmechanism_pc_kernel(
             nc.vector.tensor_reduce(out=work_of[o][:, 0:2], in_=partial[o][:], axis=AXIS.X, op=ALU.add)
 
         def sum_over_partitions(o):
-            work = work_of[o]
-            sums = psum.tile([P, 2], F32, tag="second", name="sums")
-            nc.tensor.matmul(out=sums[:, 0:1], lhsT=ones[:], rhs=work[:, 0:1], start=True, stop=True)
-            nc.tensor.matmul(out=sums[:, 1:2], lhsT=mean_weight[:], rhs=work[:, 0:1], start=True, stop=True)
+            mean = psum.tile([P, 1], F32, tag="second", name="mean")
+            nc.tensor.matmul(out=mean[:], lhsT=over_divisor[:], rhs=work_of[o][:, 0:1], start=True, stop=True)
             squares = psum.tile([P, 1], F32, tag="second", name="squares")
-            nc.tensor.matmul(out=squares[:], lhsT=square_weight[:], rhs=work[:, 1:2], start=True, stop=False)
-            nc.tensor.matmul(out=squares[:], lhsT=square_weight[:], rhs=last_square[o][:], start=False, stop=True)
-            totals[o] = sums, squares
+            parts = [work_of[o][:, 1:2], last_squares[o][:, 0:1], last_squares[o][:, 1:2]]
+            for i, part in enumerate(parts):
+                nc.tensor.matmul(out=squares[:], lhsT=over_divisor[:], rhs=part, start=(i == 0), stop=(i == 2))
+            totals[o] = mean, squares
 
         def standard_deviation(o):
             work = work_of[o]
-            sums, squares = totals[o]
-            nc.vector.tensor_copy(out=work[:, 2:4], in_=sums[:])
-            nc.vector.tensor_tensor(out=work[:, 4:5], in0=work[:, 2:3], in1=work[:, 3:4], op=ALU.mult)
+            mean, squares = totals[o]
+            nc.vector.tensor_scalar(
+                out=work[:, 2:3], in0=mean[:], scalar1=-(COUNT - 1) / COUNT, scalar2=None, op0=ALU.mult
+            )
+            nc.vector.tensor_tensor(out=work[:, 4:5], in0=mean[:], in1=work[:, 2:3], op=ALU.mult)
             nc.vector.tensor_scalar(
                 out=work[:, 5:6], in0=squares[:], scalar1=work[:, 4:5], scalar2=0.0, op0=ALU.add, op1=ALU.max
             )
@@ -407,9 +404,15 @@ def tile_retentionmechanism_pc_kernel(
                 sum_over_partitions(1)
             if step == out2_squared + 2:
                 factor(1, std)
+                factor1 = consts.tile([P, 1], F32)
+                nc.vector.tensor_tensor(out=factor1[:], in0=work_of[1][:, 7:8], in1=gate_target[:, 1:2], op=ALU.mult)
                 scale_and_store(1, nc.gpsimd, range(0, G_TILES), out_1)
-        scale_and_store(1, nc.vector, range(G_TILES, ROW_TILES), out_1)
         sum_within_partitions(0)
         sum_over_partitions(0)
-        factor(0, standard_deviation(0))
+        scale_and_store(1, nc.vector, range(G_TILES, ROW_TILES - 1), out_1)
+        std = standard_deviation(0)
+        piece = z_of[1][:, ROW_TILES - 1, :]
+        nc.scalar.activation(out=piece, in_=piece, func=ACT.Copy, scale=factor1[:])
+        nc.sync.dma_start(out=by_row_tile(out_1)[:, ROW_TILES - 1, :], in_=piece)
+        factor(0, std)
         scale_and_store(0, nc.vector, range(ROW_TILES), out1_dram)

@@ -184,12 +184,19 @@ def tile_retentionmechanism_pc_kernel(
                 in_=grouped[:, l].rearrange("p g i t -> p (g i t)"),
             )
 
+        def keep_tensor_busy(count):
+            idle = psum.tile([P, BLOCK], F32, tag="first", name="idle")
+            for i in range(count):
+                nc.tensor.matmul(out=idle[:], lhsT=wo_sb[:, 0, 0:P], rhs=wo_sb[:, 0, 0:BLOCK], start=True, stop=True)
+
         wo_grouped = new_x_grouped()
         for l in range(SLICES):
             empty_transposes(nc.scalar.copy, transpose_w_out_slice(0, l, "first"), wo_grouped, l)
+        keep_tensor_busy(2)
         next_flipped = {}
         for l in range(SLICES):
             next_flipped[l] = transpose_w_out_slice(1, l, "second")
+        keep_tensor_busy(5)
         for g in range(PASSES):
             normalise_rows(g)
             regroup_a(nc.vector.tensor_copy, 0, g)
@@ -232,11 +239,11 @@ def tile_retentionmechanism_pc_kernel(
         z_of = {1: z2}
         weight_of = {0: v_sb, 1: wo_sb}
         partial = {}
-        last_squares = {}
+        last_square = {}
         for o in range(2):
             partial[o] = consts.tile([P, 2, 2 * BANKS], F32, name="partial%d" % o)
             nc.gpsimd.memset(partial[o][:], 0.0)
-            last_squares[o] = consts.tile([P, 2], F32, name="last_squares%d" % o)
+            last_square[o] = consts.tile([P, 1], F32, name="last_square%d" % o)
         n_grouped = {}
         n_codes = {}
         n_scales = {}
@@ -314,7 +321,7 @@ def tile_retentionmechanism_pc_kernel(
                     sq_s = stage.tile([P, 2 * BLOCK], BF16, tag="sq_s", bufs=3)
                     nc.scalar.activation(
                         out=sq_s[:, 0:BLOCK], in_=z_of[o][:, r, cols], func=ACT.Square,
-                        accum_out=last_squares[o][:, col : col + 1],
+                        accum_out=last_square[o][:] if col else partial[o][:, 1, n_th : n_th + 1],
                     )
                 return
             sq_s = stage.tile([P, 2 * BLOCK], BF16, tag="sq_s", bufs=3)
@@ -331,28 +338,29 @@ def tile_retentionmechanism_pc_kernel(
         totals = {}
         work_of = {}
 
-        def sum_within_partitions(o):
-            work_of[o] = consts.tile([P, 8], F32, name="work%d" % o)
-            nc.vector.tensor_reduce(out=work_of[o][:, 0:2], in_=partial[o][:], axis=AXIS.X, op=ALU.add)
+        def sum_within_partitions(o, row):
+            if row == 0:
+                work_of[o] = consts.tile([P, 8], F32, name="work%d" % o)
+            nc.vector.tensor_reduce(out=work_of[o][:, row : row + 1], in_=partial[o][:, row, :], axis=AXIS.X, op=ALU.add)
 
-        def sum_over_partitions(o):
-            mean = psum.tile([P, 1], F32, tag="second", name="mean")
-            nc.tensor.matmul(out=mean[:], lhsT=over_divisor[:], rhs=work_of[o][:, 0:1], start=True, stop=True)
-            squares = psum.tile([P, 1], F32, tag="second", name="squares")
-            parts = [work_of[o][:, 1:2], last_squares[o][:, 0:1], last_squares[o][:, 1:2]]
+        def sum_over_partitions(o, row):
+            total = psum.tile([P, 1], F32, tag="second", name="total")
+            parts = [work_of[o][:, row : row + 1]] + [last_square[o][:]] * row
             for i, part in enumerate(parts):
-                nc.tensor.matmul(out=squares[:], lhsT=over_divisor[:], rhs=part, start=(i == 0), stop=(i == 2))
-            totals[o] = mean, squares
+                nc.tensor.matmul(out=total[:], lhsT=over_divisor[:], rhs=part, start=(i == 0), stop=(i == row))
+            totals[o, row] = total
+
+        def mean_term(o):
+            work = work_of[o]
+            nc.vector.tensor_scalar(
+                out=work[:, 2:3], in0=totals[o, 0][:], scalar1=-(COUNT - 1) / COUNT, scalar2=None, op0=ALU.mult
+            )
+            nc.vector.tensor_tensor(out=work[:, 4:5], in0=totals[o, 0][:], in1=work[:, 2:3], op=ALU.mult)
 
         def standard_deviation(o):
             work = work_of[o]
-            mean, squares = totals[o]
             nc.vector.tensor_scalar(
-                out=work[:, 2:3], in0=mean[:], scalar1=-(COUNT - 1) / COUNT, scalar2=None, op0=ALU.mult
-            )
-            nc.vector.tensor_tensor(out=work[:, 4:5], in0=mean[:], in1=work[:, 2:3], op=ALU.mult)
-            nc.vector.tensor_scalar(
-                out=work[:, 5:6], in0=squares[:], scalar1=work[:, 4:5], scalar2=0.0, op0=ALU.add, op1=ALU.max
+                out=work[:, 5:6], in0=totals[o, 1][:], scalar1=work[:, 4:5], scalar2=0.0, op0=ALU.add, op1=ALU.max
             )
             std = consts.tile([P, 1], F32, name="std%d" % o)
             nc.gpsimd.tensor_tensor(out=std[:], in0=work[:, 5:6], in1=half[:], op=ALU.pow)
@@ -381,8 +389,10 @@ def tile_retentionmechanism_pc_kernel(
             if to_square >= 0 and to_square % 2 == 1:
                 square_two_banks(to_square)
             if step == out2_squared + 1:
-                sum_within_partitions(1)
+                sum_within_partitions(1, 0)
+                sum_within_partitions(1, 1)
             if step == out2_squared + 2:
+                mean_term(1)
                 std = standard_deviation(1)
             if step == LAG:
                 wo_grouped = new_x_grouped()
@@ -401,15 +411,20 @@ def tile_retentionmechanism_pc_kernel(
             if step < total_banks and step % SLICES == SLICES - 1:
                 quantise_n(step)
             if step == out2_squared + 1:
-                sum_over_partitions(1)
+                sum_over_partitions(1, 0)
+                sum_over_partitions(1, 1)
             if step == out2_squared + 2:
                 factor(1, std)
                 factor1 = consts.tile([P, 1], F32)
                 nc.vector.tensor_tensor(out=factor1[:], in0=work_of[1][:, 7:8], in1=gate_target[:, 1:2], op=ALU.mult)
                 scale_and_store(1, nc.gpsimd, range(0, G_TILES), out_1)
-        sum_within_partitions(0)
-        sum_over_partitions(0)
-        scale_and_store(1, nc.vector, range(G_TILES, ROW_TILES - 1), out_1)
+        sum_within_partitions(0, 0)
+        sum_over_partitions(0, 0)
+        scale_and_store(1, nc.vector, range(G_TILES, G_TILES + 1), out_1)
+        sum_within_partitions(0, 1)
+        sum_over_partitions(0, 1)
+        mean_term(0)
+        scale_and_store(1, nc.vector, range(G_TILES + 1, ROW_TILES - 1), out_1)
         std = standard_deviation(0)
         piece = z_of[1][:, ROW_TILES - 1, :]
         nc.scalar.activation(out=piece, in_=piece, func=ACT.Copy, scale=factor1[:])

@@ -27,8 +27,8 @@ EPS_RMS = 1.1920929e-07
 EPS_STD = 1e-08
 COUNT = E * E
 TARGET_STD = 512.0 ** -0.5
-REGROUP_STEPS = {8: (2, 0), 10: (2, 1), 14: (3, 0), 17: (3, 1)}
-QUANTISE_STEPS = {12: 2, 20: 3}
+REGROUP_STEPS = {9: (2, 0), 11: (2, 1), 15: (3, 0), 18: (3, 1)}
+QUANTISE_STEPS = {13: 2, 21: 3}
 G_TILES = 5
 LAG = 2
 SQUARE_LAG = 3
@@ -92,18 +92,18 @@ def tile_retentionmechanism_pc_kernel(
                 in_=out_w_scales[:, 4 * quad : 4 * quad + 4, :].rearrange("g r n -> r g n").bitcast(I32),
             )
 
-        vq_sb = keep.tile([P, PASSES, 2, 2, E], BF16)
-        v_rows = by_word_order(v_dram)
-        for g in range(PASSES):
-            for u in range(2):
-                nc.sync.dma_start(out=vq_sb[:, g, u], in_=v_rows[g, u])
-
         w_codes = keep.tile([P, PASSES, E], U32, align_bytes=64)
         for g2 in range(PASSES):
             nc.sync.dma_start(
                 out=w_codes[:, g2, :].bitcast(I32),
                 in_=out_w_words[g2].rearrange("p n t -> p (n t)").bitcast(I32),
             )
+
+        vq_sb = keep.tile([P, PASSES, 2, 2, E], BF16)
+        v_rows = by_word_order(v_dram)
+        for g in range(PASSES):
+            for u in range(2):
+                nc.sync.dma_start(out=vq_sb[:, g, u], in_=v_rows[g, u])
 
         v_sb = keep.tile([P, ROW_TILES, E], BF16)
         v_tiles = by_row_tile(v_dram)
@@ -184,28 +184,25 @@ def tile_retentionmechanism_pc_kernel(
                 in_=grouped[:, l].rearrange("p g i t -> p (g i t)"),
             )
 
-        def keep_tensor_busy(count):
-            idle = psum.tile([P, BLOCK], F32, tag="first", name="idle")
-            for i in range(count):
-                nc.tensor.matmul(out=idle[:], lhsT=wo_sb[:, 0, 0:P], rhs=wo_sb[:, 0, 0:BLOCK], start=True, stop=True)
-
         wo_grouped = new_x_grouped()
         for l in range(SLICES):
             empty_transposes(nc.scalar.copy, transpose_w_out_slice(0, l, "first"), wo_grouped, l)
-        keep_tensor_busy(2)
+        next_grouped = new_x_grouped()
         next_flipped = {}
         for l in range(SLICES):
             next_flipped[l] = transpose_w_out_slice(1, l, "second")
-        keep_tensor_busy(5)
         for g in range(PASSES):
             normalise_rows(g)
             regroup_a(nc.vector.tensor_copy, 0, g)
+        regroup_a(nc.scalar.copy, 1, 0)
+        for l in range(4):
+            empty_transposes(nc.scalar.copy, next_flipped[l], next_grouped, l)
         quantise_x_slice(0, 0, wo_grouped)
         for g in range(PASSES):
             quantise_a(0, g)
-        for g in range(PASSES):
-            regroup_a(nc.scalar.copy, 1, g)
-        for l in range(1, SLICES):
+        quantise_x_slice(0, 1, wo_grouped)
+        regroup_a(nc.vector.tensor_copy, 1, 1)
+        for l in range(2, SLICES):
             quantise_x_slice(0, l, wo_grouped)
         for g in range(PASSES):
             quantise_a(1, g)
@@ -395,11 +392,8 @@ def tile_retentionmechanism_pc_kernel(
                 mean_term(1)
                 std = standard_deviation(1)
             if step == LAG:
-                wo_grouped = new_x_grouped()
                 for l in range(SLICES):
-                    empty_transposes(nc.vector.tensor_copy, next_flipped[l], wo_grouped, l)
-                for l in range(SLICES):
-                    quantise_x_slice(1, l, wo_grouped)
+                    quantise_x_slice(1, l, next_grouped)
             if step in REGROUP_STEPS:
                 regroup_v(*REGROUP_STEPS[step])
             if step in QUANTISE_STEPS:

from contextlib import ExitStack

import concourse.mybir as mybir
from concourse.masks import make_identity

FP8X4 = mybir.dt.float8_e4m3fn_x4
BF16 = mybir.dt.bfloat16
F32 = mybir.dt.float32
I32 = mybir.dt.int32
U32 = mybir.dt.uint32
U8 = mybir.dt.uint8
ACT = mybir.ActivationFunctionType
ALU = mybir.AluOpType
AXIS = mybir.AxisListType

P = 128
E = 1024
PACK = 4
K_PASS = P * PACK
PASSES = E // K_PASS
BLOCK = 512
SLICES = BLOCK // P
BLOCKS = 2 * E // BLOCK
BANKS = SLICES * PASSES
ROW_TILES = E // P
EPS_RMS = 1.1920929e-07
EPS_STD = 1e-08
COUNT = E * E
TARGET_STD = 512.0 ** -0.5
REGROUP_STEPS = {9: (2, 0), 11: (2, 1), 15: (3, 0), 18: (3, 1)}
QUANTISE_STEPS = {13: 2, 21: 3}
G_TILES = 5
LAG = 2
SQUARE_LAG = 3

FLOPS = 4 * 2 * E * E * E


def tile_retentionmechanism_pc_kernel(
    tc, ao, w_swiglu, w_out, out_w_words, out_w_scales, tao, out_0, out_1
):
    nc = tc.nc
    with ExitStack() as ctx:
        ctx.enter_context(tc.manual_schedule())
        consts = ctx.enter_context(tc.tile_pool(name="consts", bufs=1))
        keep = ctx.enter_context(tc.tile_pool(name="keep", bufs=1))
        stage = ctx.enter_context(tc.tile_pool(name="stage", bufs=2))
        psum = ctx.enter_context(tc.psum_pool(name="psum", bufs=4))

        v_dram = w_swiglu.rearrange("(d h) q -> d (h q)", h=2)
        out1_dram = out_0.rearrange("(d h) q -> d (h q)", h=2)

        def by_word_order(x):
            return x.rearrange("(g u p h) c -> g u p h c", g=PASSES, u=2, p=P, h=2)

        def by_row_tile(x):
            return x.rearrange("(r p) c -> p r c", p=P)

        half = consts.tile([P, 1], F32)
        nc.gpsimd.memset(half[:], 0.5)
        minus_half = consts.tile([P, 2, 2], F32)
        nc.gpsimd.memset(minus_half[:], -0.5)
        ident = consts.tile([P, P], F32)
        make_identity(nc, ident[:])
        over_divisor = consts.tile([P, P], F32)
        nc.gpsimd.memset(over_divisor[:], 1.0 / (COUNT - 1))
        warm = consts.tile([P, 1], F32)
        nc.scalar.activation(out=warm[:], in_=half[:], func=ACT.Silu)

        head = keep.tile([P, 2 * PASSES * PACK * E], BF16, tag="big", align_bytes=64)
        ao_sb = head[:, 0 : PASSES * PACK * E].rearrange("p (g u h c) -> p g u h c", g=PASSES, u=2, h=2)
        a_grouped = head[:, PASSES * PACK * E :].rearrange("p (g2 g x) -> p g2 g x", g2=PASSES, g=PASSES)
        ao_rows = by_word_order(ao)
        for g in range(PASSES):
            for u in range(2):
                nc.sync.dma_start(out=ao_sb[:, g, u], in_=ao_rows[g, u])

        tao_sb = consts.tile([P, 2], BF16)
        nc.scalar.dma_start(out=tao_sb[:], in_=tao.rearrange("a b -> (a b)").partition_broadcast(P))

        wo_sb = keep.tile([P, ROW_TILES, E], BF16)
        wo_rows = by_row_tile(w_out)

        for r in range(0, ROW_TILES, 2):
            nc.sync.dma_start(out=wo_sb[:, r : r + 2, :], in_=wo_rows[:, r : r + 2, :])

        w_scales = keep.tile([P, PASSES, E], U8, align_bytes=64)
        nc.vector.memset(w_scales[:].rearrange("p g n -> p (g n)").bitcast(I32), 0)
        for quad in range(4):
            nc.sync.dma_start(
                out=w_scales[32 * quad : 32 * quad + 4].bitcast(I32),
                in_=out_w_scales[:, 4 * quad : 4 * quad + 4, :].rearrange("g r n -> r g n").bitcast(I32),
            )

        w_codes = keep.tile([P, PASSES, E], U32, align_bytes=64)
        for g2 in range(PASSES):
            nc.sync.dma_start(
                out=w_codes[:, g2, :].bitcast(I32),
                in_=out_w_words[g2].rearrange("p n t -> p (n t)").bitcast(I32),
            )

        vq_sb = keep.tile([P, PASSES, 2, 2, E], BF16)
        v_rows = by_word_order(v_dram)
        for g in range(PASSES):
            for u in range(2):
                nc.sync.dma_start(out=vq_sb[:, g, u], in_=v_rows[g, u])

        v_sb = keep.tile([P, ROW_TILES, E], BF16)
        v_tiles = by_row_tile(v_dram)
        for r in range(0, ROW_TILES, 2):
            nc.sync.dma_start(out=v_sb[:, r : r + 2, :], in_=v_tiles[:, r : r + 2, :])

        sumsq = consts.tile([P, 2, 8], F32)
        mean_sq = consts.tile([P, 2, 8], F32)
        rstd = consts.tile([P, 2, 8], F32)
        for g in range(PASSES):
            for u in range(2):
                col = 2 * g + u
                sq_s = stage.tile([P, E], BF16, tag="sq_s", bufs=3)
                nc.scalar.activation(
                    out=sq_s[:], in_=ao_sb[:, g, u, 0, :], func=ACT.Square,
                    accum_out=sumsq[:, 0, col : col + 1],
                )
                sq_v = stage.tile([P, E], BF16, tag="sq_v")
                nc.vector.scalar_tensor_tensor(
                    out=sq_v[:], in0=ao_sb[:, g, u, 1, :], scalar=1.0, in1=ao_sb[:, g, u, 1, :],
                    op0=ALU.mult, op1=ALU.mult, accum_out=sumsq[:, 1, col : col + 1],
                )
            pair = slice(2 * g, 2 * g + 2)
            nc.gpsimd.tensor_scalar(
                out=mean_sq[:, :, pair], in0=sumsq[:, :, pair],
                scalar1=1.0 / E, scalar2=EPS_RMS, op0=ALU.mult, op1=ALU.add,
            )
            nc.gpsimd.tensor_tensor(out=rstd[:, :, pair], in0=mean_sq[:, :, pair], in1=minus_half[:], op=ALU.pow)

        a_codes = keep.tile([P, PASSES, PASSES, K_PASS], U32, align_bytes=64)
        a_scales = keep.tile([P, PASSES, PASSES, K_PASS], U8, align_bytes=64)

        def normalise_rows(g):
            for u in range(2):
                for h in range(2):
                    nc.vector.tensor_scalar(
                        out=ao_sb[:, g, u, h, :], in0=ao_sb[:, g, u, h, :],
                        scalar1=rstd[:, h, 2 * g + u : 2 * g + u + 1], scalar2=None, op0=ALU.mult,
                    )

        def regroup_a(copy, g2, g):
            rows = ao_sb[:, g].rearrange("p u h c -> p (u h) c")[:, :, g2 * K_PASS : (g2 + 1) * K_PASS]
            copy(
                out=a_grouped[:, g2, g, :].rearrange("p (s c t) -> p c t s", s=PACK, t=PACK),
                in_=rows.rearrange("p t (c s) -> p c t s", s=PACK),
            )

        def quantise_a(g2, g):
            nc.vector.quantize_mx(
                out=a_codes[:, g2, g, :].bitcast(FP8X4), scales=a_scales[:, g2, g, :],
                in_=a_grouped[:, g2, g, :],
            )

        x_codes = keep.tile([P, BLOCKS, SLICES, PASSES, P], U32, align_bytes=64)
        x_scales = keep.tile([P, BLOCKS, SLICES, PASSES, P], U8, align_bytes=64)

        def new_x_grouped():
            x_grouped = stage.tile([P, SLICES, PASSES, P, PACK], BF16, tag="x_grouped", bufs=3, align_bytes=64)
            return x_grouped

        def transpose_w_out_slice(blk, l, bank_tag):
            words = wo_sb[:, blk * SLICES + l, :].bitcast(F32)
            flipped = psum.tile([P, PACK, P], F32, tag=bank_tag, name="flipped")
            for b in range(PACK):
                nc.tensor.transpose(flipped[:, b, :], words[:, b * P : (b + 1) * P], ident[:])
            return flipped

        def empty_transposes(copy, flipped, grouped, l):
            copy(
                out=grouped[:, l].rearrange("p g i t -> p g (i t)").bitcast(F32).rearrange("p g (i u) -> p g i u", u=2),
                in_=flipped[:].rearrange("p (g u) i -> p g i u", u=2),
            )

        def quantise_x_slice(blk, l, grouped):
            nc.vector.quantize_mx(
                out=x_codes[:, blk, l].rearrange("p g c -> p (g c)").bitcast(FP8X4),
                scales=x_scales[:, blk, l].rearrange("p g c -> p (g c)"),
                in_=grouped[:, l].rearrange("p g i t -> p (g i t)"),
            )

        wo_grouped = new_x_grouped()
        for l in range(SLICES):
            empty_transposes(nc.scalar.copy, transpose_w_out_slice(0, l, "first"), wo_grouped, l)
        next_grouped = new_x_grouped()
        next_flipped = {}
        for l in range(SLICES):
            next_flipped[l] = transpose_w_out_slice(1, l, "second")
        for g in range(PASSES):
            normalise_rows(g)
            regroup_a(nc.vector.tensor_copy, 0, g)
        regroup_a(nc.scalar.copy, 1, 0)
        for l in range(4):
            empty_transposes(nc.scalar.copy, next_flipped[l], next_grouped, l)
        quantise_x_slice(0, 0, wo_grouped)
        for g in range(PASSES):
            quantise_a(0, g)
        quantise_x_slice(0, 1, wo_grouped)
        regroup_a(nc.vector.tensor_copy, 1, 1)
        for l in range(2, SLICES):
            quantise_x_slice(0, l, wo_grouped)
        for g in range(PASSES):
            quantise_a(1, g)

        gate = consts.tile([P, 2], F32)
        nc.vector.tensor_scalar(out=gate[:], in0=tao_sb[:], scalar1=-1.0, scalar2=None, op0=ALU.mult)
        nc.vector.tensor_tensor(out=gate[:], in0=gate[:], in1=tao_sb[:], op=ALU.max)
        nc.vector.tensor_scalar(out=gate[:], in0=gate[:], scalar1=1e-08, scalar2=1.0, op0=ALU.max, op1=ALU.min)
        gate_target = consts.tile([P, 2], F32)
        nc.vector.tensor_scalar(out=gate_target[:], in0=gate[:], scalar1=TARGET_STD, scalar2=None, op0=ALU.mult)

        v_grouped = {}

        def regroup_v(blk, g):
            if g == 0:
                v_grouped[blk] = new_x_grouped()
            rows = vq_sb[:, g].rearrange("p u h c -> p (u h) c")[:, :, (blk - 2) * BLOCK : (blk - 1) * BLOCK]
            nc.vector.tensor_copy(
                out=v_grouped[blk][:, :, g, :, :].rearrange("p l (c i) t -> p l c t i", i=4),
                in_=rows.rearrange("p t (l c i) -> p l c t i", l=SLICES, i=4),
            )

        def quantise_v_block(blk):
            nc.vector.quantize_mx(
                out=x_codes[:, blk].rearrange("p l g c -> p (l g c)").bitcast(FP8X4),
                scales=x_scales[:, blk].rearrange("p l g c -> p (l g c)"),
                in_=v_grouped[blk][:].rearrange("p l g c t -> p (l g c t)"),
            )

        z2 = keep.tile([P, ROW_TILES, E], F32)
        z_of = {1: z2}
        weight_of = {0: v_sb, 1: wo_sb}
        partial = {}
        last_square = {}
        for o in range(2):
            partial[o] = consts.tile([P, 2, 2 * BANKS], F32, name="partial%d" % o)
            nc.gpsimd.memset(partial[o][:], 0.0)
            last_square[o] = consts.tile([P, 1], F32, name="last_square%d" % o)
        n_grouped = {}
        n_codes = {}
        n_scales = {}

        def first_product_bank(k):
            blk, g2, cb = k // BANKS, (k % BANKS) // SLICES, k % SLICES
            if k % BANKS == 0:
                n_grouped[blk] = stage.tile([P, PASSES, BLOCK, PACK], BF16, tag="n_grouped", name="n_grouped", align_bytes=64)
                n_codes[blk] = stage.tile([P, PASSES, BLOCK], U32, tag="n_codes", name="n_codes", bufs=3, align_bytes=64)
                n_scales[blk] = stage.tile([P, PASSES, BLOCK], U8, tag="n_scales", name="n_scales", bufs=3, align_bytes=64)
            bank = psum.tile([P, PACK, P], F32, tag="first")
            for s in range(PACK):
                for g in range(PASSES):
                    nc.tensor.matmul_mx(
                        out=bank[:, s, :],
                        lhsT=a_codes[:, g2, g, s * P : (s + 1) * P].bitcast(FP8X4),
                        lhsT_scale=a_scales[:, g2, g, s * P : (s + 1) * P],
                        rhs=x_codes[:, blk, cb, g, :].bitcast(FP8X4),
                        rhs_scale=x_scales[:, blk, cb, g, :],
                        start=(g == 0),
                        stop=(g == PASSES - 1),
                    )
            nc.scalar.activation(
                out=n_grouped[blk][:, g2, cb * P : (cb + 1) * P, :], in_=bank[:].rearrange("p s c -> p c s"), func=ACT.Silu
            )

        def quantise_n(k):
            blk, g2 = k // BANKS, (k % BANKS) // SLICES
            nc.vector.quantize_mx(
                out=n_codes[blk][:, g2, :].bitcast(FP8X4), scales=n_scales[blk][:, g2, :],
                in_=n_grouped[blk][:, g2].rearrange("p c s -> p (c s)"),
            )

        def place_of_bank(k):
            blk, b = k // BANKS, k % BANKS
            if blk < 2:
                return 1, blk * SLICES + b // 2, slice((b % 2) * BLOCK, (b % 2 + 1) * BLOCK)
            return 0, b, slice((blk - 2) * BLOCK, (blk - 1) * BLOCK)

        def second_product_bank(k):
            blk, b = k // BANKS, k % BANKS
            o, r, cols = place_of_bank(k)
            bank = psum.tile([P, BLOCK], F32, tag="second")
            for g2 in range(PASSES):
                if o == 1:
                    inner = slice((b // 2) * P, (b // 2 + 1) * P)
                    nc.tensor.matmul_mx(
                        out=bank[:],
                        lhsT=n_codes[blk][:, g2, inner].bitcast(FP8X4), lhsT_scale=n_scales[blk][:, g2, inner],
                        rhs=w_codes[:, g2, cols].bitcast(FP8X4), rhs_scale=w_scales[:, g2, cols],
                        start=(g2 == 0), stop=(g2 == PASSES - 1),
                    )
                else:
                    inner = slice(r * P, (r + 1) * P)
                    nc.tensor.matmul_mx(
                        out=bank[:],
                        lhsT=w_codes[:, g2, inner].bitcast(FP8X4), lhsT_scale=w_scales[:, g2, inner],
                        rhs=n_codes[blk][:, g2, :].bitcast(FP8X4), rhs_scale=n_scales[blk][:, g2, :],
                        start=(g2 == 0), stop=(g2 == PASSES - 1),
                    )
            if k == 2 * BANKS:
                z_of[0] = keep.tile([P, ROW_TILES, E], F32, tag="big", name="z1", align_bytes=64)
            n_th = k % (2 * BANKS)
            nc.vector.scalar_tensor_tensor(
                out=z_of[o][:, r, cols], in0=bank[:], scalar=1.0, in1=weight_of[o][:, r, cols],
                op0=ALU.mult, op1=ALU.add, accum_out=partial[o][:, 0, n_th : n_th + 1],
            )

        def square_two_banks(k):
            o, r, cols = place_of_bank(k)
            n_th = (k % (2 * BANKS)) // 2
            if n_th == BANKS - 1:
                for col, bank in ((0, k - 1), (1, k)):
                    o, r, cols = place_of_bank(bank)
                    sq_s = stage.tile([P, 2 * BLOCK], BF16, tag="sq_s", bufs=3)
                    nc.scalar.activation(
                        out=sq_s[:, 0:BLOCK], in_=z_of[o][:, r, cols], func=ACT.Square,
                        accum_out=last_square[o][:] if col else partial[o][:, 1, n_th : n_th + 1],
                    )
                return
            sq_s = stage.tile([P, 2 * BLOCK], BF16, tag="sq_s", bufs=3)
            if o == 1:
                nc.scalar.activation(
                    out=sq_s[:], in_=z_of[o][:, r, :], func=ACT.Square, accum_out=partial[o][:, 1, n_th : n_th + 1]
                )
            else:
                nc.scalar.activation(
                    out=sq_s[:].rearrange("p (a c) -> p a c", a=2), in_=z_of[o][:, r - 1 : r + 1, cols], func=ACT.Square,
                    accum_out=partial[o][:, 1, n_th : n_th + 1],
                )

        totals = {}
        work_of = {}

        def sum_within_partitions(o, row):
            if row == 0:
                work_of[o] = consts.tile([P, 8], F32, name="work%d" % o)
            nc.vector.tensor_reduce(out=work_of[o][:, row : row + 1], in_=partial[o][:, row, :], axis=AXIS.X, op=ALU.add)

        def sum_over_partitions(o, row):
            total = psum.tile([P, 1], F32, tag="second", name="total")
            parts = [work_of[o][:, row : row + 1]] + [last_square[o][:]] * row
            for i, part in enumerate(parts):
                nc.tensor.matmul(out=total[:], lhsT=over_divisor[:], rhs=part, start=(i == 0), stop=(i == row))
            totals[o, row] = total

        def mean_term(o):
            work = work_of[o]
            nc.vector.tensor_scalar(
                out=work[:, 2:3], in0=totals[o, 0][:], scalar1=-(COUNT - 1) / COUNT, scalar2=None, op0=ALU.mult
            )
            nc.vector.tensor_tensor(out=work[:, 4:5], in0=totals[o, 0][:], in1=work[:, 2:3], op=ALU.mult)

        def standard_deviation(o):
            work = work_of[o]
            nc.vector.tensor_scalar(
                out=work[:, 5:6], in0=totals[o, 1][:], scalar1=work[:, 4:5], scalar2=0.0, op0=ALU.add, op1=ALU.max
            )
            std = consts.tile([P, 1], F32, name="std%d" % o)
            nc.gpsimd.tensor_tensor(out=std[:], in0=work[:, 5:6], in1=half[:], op=ALU.pow)
            return std

        def factor(o, std):
            work = work_of[o]
            nc.vector.tensor_scalar(out=work[:, 6:7], in0=std[:], scalar1=EPS_STD, scalar2=None, op0=ALU.add)
            nc.vector.reciprocal(out=work[:, 7:8], in_=work[:, 6:7])

        def scale_and_store(o, engine, tiles, out_dram):
            rows = by_row_tile(out_dram)
            for r in tiles:
                piece = z_of[o][:, r, :]
                engine.tensor_scalar(
                    out=piece, in0=piece, scalar1=work_of[o][:, 7:8], scalar2=gate_target[:, o : o + 1],
                    op0=ALU.mult, op1=ALU.mult,
                )
                nc.sync.dma_start(out=rows[:, r, :], in_=piece)

        total_banks = BLOCKS * BANKS
        behind = BANKS + LAG
        out2_squared = 2 * BANKS - 1 + behind + SQUARE_LAG
        for step in range(total_banks + behind + SQUARE_LAG):
            to_square = step - behind - SQUARE_LAG
            if to_square >= 0 and to_square % 2 == 1:
                square_two_banks(to_square)
            if step == out2_squared + 1:
                sum_within_partitions(1, 0)
                sum_within_partitions(1, 1)
            if step == out2_squared + 2:
                mean_term(1)
                std = standard_deviation(1)
            if step == LAG:
                for l in range(SLICES):
                    quantise_x_slice(1, l, next_grouped)
            if step in REGROUP_STEPS:
                regroup_v(*REGROUP_STEPS[step])
            if step in QUANTISE_STEPS:
                quantise_v_block(QUANTISE_STEPS[step])
            if step < total_banks:
                first_product_bank(step)
            if behind <= step < total_banks + behind:
                second_product_bank(step - behind)
            if step < total_banks and step % SLICES == SLICES - 1:
                quantise_n(step)
            if step == out2_squared + 1:
                sum_over_partitions(1, 0)
                sum_over_partitions(1, 1)
            if step == out2_squared + 2:
                factor(1, std)
                factor1 = consts.tile([P, 1], F32)
                nc.vector.tensor_tensor(out=factor1[:], in0=work_of[1][:, 7:8], in1=gate_target[:, 1:2], op=ALU.mult)
                scale_and_store(1, nc.gpsimd, range(0, G_TILES), out_1)
        sum_within_partitions(0, 0)
        sum_over_partitions(0, 0)
        scale_and_store(1, nc.vector, range(G_TILES, G_TILES + 1), out_1)
        sum_within_partitions(0, 1)
        sum_over_partitions(0, 1)
        mean_term(0)
        scale_and_store(1, nc.vector, range(G_TILES + 1, ROW_TILES - 1), out_1)
        std = standard_deviation(0)
        piece = z_of[1][:, ROW_TILES - 1, :]
        nc.scalar.activation(out=piece, in_=piece, func=ACT.Copy, scale=factor1[:])
        nc.sync.dma_start(out=by_row_tile(out_1)[:, ROW_TILES - 1, :], in_=piece)
        factor(0, std)
        scale_and_store(0, nc.vector, range(ROW_TILES), out1_dram)
